import numpy as np
import ml_dtypes


def mxq(x, axis, fmt="e4m3"):
    dtype, down = {"e4m3": (ml_dtypes.float8_e4m3fn, 7), "e5m2": (ml_dtypes.float8_e5m2, 14)}[fmt]
    v = np.moveaxis(np.asarray(x, np.float32).astype(ml_dtypes.bfloat16).astype(np.float64), axis, -1)
    blocks = v.reshape(v.shape[:-1] + (-1, 32))
    amax = np.abs(blocks).max(-1, keepdims=True)
    byte = np.maximum(np.where(amax > 0, np.frexp(amax)[1] - 1 + 127, 0) - down, 1)
    scale = np.exp2(byte - 127.0)
    codes = (blocks / scale).astype(np.float32).astype(dtype).astype(np.float64)
    return np.moveaxis((codes * scale).reshape(v.shape), -1, axis)


WIDE = False


def mx_kscale(k):
    if not WIDE:
        return np.ones(k)
    levels = np.array([10, -10, 5, -5, 0])
    a = np.random.permutation(np.resize(levels, k // 512 * 4)).reshape(k // 512, 4)
    idx = np.arange(k)
    return np.exp2(a[idx // 512, idx % 128 // 32])


BF16 = ml_dtypes.bfloat16


def bf(x):
    return np.asarray(x, np.float32).astype(BF16)


def f64(x):
    return np.asarray(x).astype(np.float64)


B, S, DIN, DOUT = 4, 2048, 1024, 256
EPS = float(np.finfo(np.float32).eps)


def setup_inputs():
    s = mx_kscale(DIN)
    return {"x": bf(np.random.standard_normal((B, S, DIN))),
            "weight": bf(np.random.standard_normal((DOUT, DIN)) * np.sqrt(2.0 / DIN) / (s * s)[None, :]),
            "bias": bf(np.random.standard_normal(DOUT) * 0.5),
            "gamma": bf((1.0 + 0.1 * np.random.standard_normal(DIN)) * 8.0 / np.sqrt(DIN) * s / s.min())}


def reference(x, weight, bias, gamma):
    x = f64(x)
    weight = f64(weight)
    ms = np.mean(x * x, axis=-1, keepdims=True)
    xn = x * (1.0 / np.sqrt(ms + EPS)) * f64(gamma)
    thr = np.mean(np.abs(weight))
    w_t = np.sign(weight) * (np.abs(weight) > thr).astype(np.float64)
    w = weight + (w_t - weight)
    out = (mxq(xn, 2, "e4m3") @ mxq(w, 1, "e4m3").T) + f64(bias)
    return out

@@ -1,0 +1,181 @@
+from contextlib import ExitStack
+
+import concourse.mybir as mybir
+from concourse.masks import make_identity
+
+FLOPS = 2 * 8192 * 1024 * 256
+
+BF16 = mybir.dt.bfloat16
+F32 = mybir.dt.float32
+U8 = mybir.dt.uint8
+U32 = mybir.dt.uint32
+FP8X4 = mybir.dt.float8_e4m3fn_x4
+ALU = mybir.AluOpType
+ACT = mybir.ActivationFunctionType
+AX = mybir.AxisListType
+
+P = 128
+DIN = 1024
+DOUT = 256
+ROWS = 8192
+EPS = 2.0 ** -23
+QUARTER = 256
+SUB_ROWS = 32
+CHUNKS = [1, 1, 2] + [4] * 14 + [2, 1, 1]
+
+
+def tile_bitlinear_t_kernel(tc, x, weight, bias, gamma, out):
+    nc = tc.nc
+    assert sum(CHUNKS) * P == ROWS
+    x_q = x.rearrange("b s (a i) -> (b s a) i", a=4).rearrange("(t q) i -> q t i", q=P)
+    out_v = out.flatten_outer_dims().rearrange("(r m) n -> m r n", m=P)
+
+    with ExitStack() as ctx:
+        const = ctx.enter_context(tc.tile_pool(name="const", bufs=1))
+        xpool = ctx.enter_context(tc.tile_pool(name="xpool", bufs=4))
+        npool = ctx.enter_context(tc.tile_pool(name="npool", bufs=3))
+        gpool = ctx.enter_context(tc.tile_pool(name="gpool", bufs=3))
+        qpool = ctx.enter_context(tc.tile_pool(name="qpool", bufs=3))
+        opool = ctx.enter_context(tc.tile_pool(name="opool", bufs=3))
+        small = ctx.enter_context(tc.tile_pool(name="small", bufs=4))
+        ps_t = ctx.enter_context(tc.psum_pool(name="ps_t", bufs=4))
+        ps_o = ctx.enter_context(tc.psum_pool(name="ps_o", bufs=2))
+        ps_s = ctx.enter_context(tc.psum_pool(name="ps_s", bufs=2))
+
+        first = CHUNKS[0] * 4
+        xs0 = xpool.tile([P, 16, QUARTER], BF16, name="xs", tag="xs")
+        nc.sync.dma_start(out=xs0[:, 0:first, :], in_=x_q[:, 0:first, :])
+        w_sb = const.tile([P, 2, DIN], BF16)
+        nc.sync.dma_start(out=w_sb[:], in_=weight.rearrange("(h p) k -> p h k", p=P))
+        gam = const.tile([P, QUARTER], BF16)
+        for a in range(4):
+            nc.scalar.dma_start(
+                out=gam[a:P:4, :],
+                in_=gamma[a * QUARTER : (a + 1) * QUARTER].partition_broadcast(SUB_ROWS),
+            )
+        bias_bf = const.tile([P, DOUT], BF16)
+        nc.scalar.dma_start(out=bias_bf[:], in_=bias.partition_broadcast(P))
+
+        warm = const.tile([P, 1], F32)
+        nc.vector.memset(warm[:], 1.0)
+        nc.scalar.activation(out=warm[:], in_=warm[:], func=ACT.Sqrt)
+        ident = const.tile([P, P], BF16)
+        make_identity(nc, ident[:])
+        identf = const.tile([P, P], F32)
+        make_identity(nc, identf[:])
+        grp = const.tile([P, 32], F32)
+        nc.vector.tensor_reduce(
+            out=grp[:], in_=identf[:].rearrange("p (g a) -> p g a", a=4), axis=AX.X, op=ALU.add
+        )
+        same_row = const.tile([P, 32, 4], F32)
+        nc.vector.tensor_copy(out=same_row[:], in_=grp[:].unsqueeze(2).to_broadcast([P, 32, 4]))
+        ones = const.tile([P, P], F32)
+        nc.vector.memset(ones[:], 1.0)
+        bias2 = const.tile([P, 2, DOUT], F32)
+        nc.vector.tensor_copy(out=bias2[:], in_=bias_bf[:].unsqueeze(1).to_broadcast([P, 2, DOUT]))
+
+        w_flat = w_sb[:].rearrange("p h k -> p (h k)")
+        w_abs = const.tile([P, 2 * DIN], BF16)
+        abs_sum = const.tile([P, 1], F32)
+        nc.vector.scalar_tensor_tensor(
+            out=w_abs[:], in0=w_flat, scalar=-1.0, in1=w_flat, op0=ALU.mult, op1=ALU.max,
+            accum_out=abs_sum[:],
+        )
+        tot = ps_s.tile([P, 1], F32, tag="ps")
+        nc.tensor.matmul(tot[:], lhsT=ones[:], rhs=abs_sum[:], start=True, stop=True)
+        thr = const.tile([P, 1], F32)
+        nc.vector.tensor_scalar(out=thr[:], in0=tot[:], scalar1=1.0 / (DOUT * DIN), scalar2=None, op0=ALU.mult)
+        nthr = const.tile([P, 1], F32)
+        nc.vector.tensor_scalar(out=nthr[:], in0=tot[:], scalar1=-1.0 / (DOUT * DIN), scalar2=None, op0=ALU.mult)
+        w_neg = const.tile([P, 2 * DIN], BF16)
+        nc.vector.tensor_scalar(out=w_neg[:], in0=w_flat, scalar1=nthr[:, 0:1], scalar2=None, op0=ALU.is_lt)
+        w_t = const.tile([P, 2, DIN], BF16)
+        nc.vector.scalar_tensor_tensor(
+            out=w_t[:].rearrange("p h k -> p (h k)"), in0=w_flat, scalar=thr[:, 0:1], in1=w_neg[:],
+            op0=ALU.is_gt, op1=ALU.subtract,
+        )
+        w_grouped = const.tile([P, 2, DOUT, 4], BF16, align_bytes=64)
+        for h in range(2):
+            w_ps = ps_t.tile([P, 8, P], BF16, tag="pt")
+            for kb in range(8):
+                nc.tensor.transpose(out=w_ps[:, kb, :], in_=w_t[:, h, kb * P : (kb + 1) * P], identity=ident[:])
+            for g in range(2):
+                nc.vector.tensor_copy(
+                    out=w_grouped[:, g, h * P : (h + 1) * P, :].rearrange("c n (b a) -> c n b a", b=2),
+                    in_=w_ps[:, 4 * g : 4 * g + 4, :].rearrange("c (a b) n -> c n b a", a=2),
+                )
+        w_codes = const.tile([P, 2 * DOUT], U32, align_bytes=64)
+        w_scales = const.tile([P, 2 * DOUT], U8, align_bytes=64)
+        nc.vector.quantize_mx(
+            out=w_codes[:].bitcast(FP8X4), scales=w_scales[:],
+            in_=w_grouped[:].rearrange("c g n j -> c (g n j)"),
+        )
+
+        row_tile = 0
+        for ci, n_rt in enumerate(CHUNKS):
+            n_sub = 4 * n_rt
+            t0 = 4 * row_tile
+            if ci == 0:
+                xs = xs0
+            else:
+                xs = xpool.tile([P, 16, QUARTER], BF16, name="xs", tag="xs")
+                nc.sync.dma_start(out=xs[:, 0:n_sub, :], in_=x_q[:, t0 : t0 + n_sub, :])
+            ssq = small.tile([P, 16], F32)
+            for t in range(n_sub):
+                sq = small.tile([P, QUARTER], BF16)
+                nc.scalar.activation(out=sq[:], in_=xs[:, t, :], func=ACT.Square, accum_out=ssq[:, t : t + 1])
+            ms = ps_s.tile([P, 16], F32, tag="ps")
+            nc.tensor.matmul(
+                ms[:, 0:n_sub], lhsT=same_row[:].rearrange("p g a -> p (g a)"), rhs=ssq[:, 0:n_sub],
+                start=True, stop=True,
+            )
+            std = small.tile([P, 16], F32)
+            nc.scalar.activation(out=std[:, 0:n_sub], in_=ms[:, 0:n_sub], func=ACT.Sqrt, scale=1.0 / DIN, bias=EPS)
+            rstd = small.tile([P, 16], F32)
+            nc.vector.reciprocal(out=rstd[:, 0:n_sub], in_=std[:, 0:n_sub])
+            xn = npool.tile([P, 16, QUARTER], BF16)
+            for t in range(n_sub):
+                nc.vector.scalar_tensor_tensor(
+                    out=xn[:, t, :], in0=xs[:, t, :], scalar=rstd[:, t : t + 1], in1=gam[:],
+                    op0=ALU.mult, op1=ALU.mult,
+                )
+            grouped = gpool.tile([P, 4, 2, P, 4], BF16, align_bytes=64)
+            for r in range(n_rt):
+                pt = ps_t.tile([P, 2, P, 4], BF16, tag="pt")
+                for s in range(4):
+                    for b in range(2):
+                        nc.tensor.transpose(
+                            out=pt[:, :, 32 * s : 32 * s + 32, 2 * b : 2 * b + 2].rearrange("c g w a -> c w g a"),
+                            in_=xn[:, 4 * r + s, b * P : (b + 1) * P],
+                            identity=ident[:],
+                        )
+                nc.scalar.copy(
+                    out=grouped[:, r].rearrange("c g m j -> c (g m j)"),
+                    in_=pt[:].rearrange("c g m j -> c (g m j)"),
+                )
+            codes = qpool.tile([P, 4 * 2 * P], U32, align_bytes=64)
+            scales = qpool.tile([P, 4 * 2 * P], U8, align_bytes=64)
+            width = n_rt * 2 * P
+            nc.vector.quantize_mx(
+                out=codes[:, 0:width].bitcast(FP8X4), scales=scales[:, 0:width],
+                in_=grouped[:, 0:n_rt].rearrange("c r g m j -> c (r g m j)"),
+            )
+            o_sb = opool.tile([P, 4, DOUT], F32)
+            for r0 in range(0, n_rt, 2):
+                pair = min(2, n_rt - r0)
+                po = ps_o.tile([P, 2, DOUT], F32)
+                for r in range(r0, r0 + pair):
+                    for g in range(2):
+                        cols = slice((2 * r + g) * P, (2 * r + g + 1) * P)
+                        nc.tensor.matmul_mx(
+                            out=po[:, r - r0, :],
+                            lhsT=codes[:, cols].bitcast(FP8X4), lhsT_scale=scales[:, cols],
+                            rhs=w_codes[:, g * DOUT : (g + 1) * DOUT].bitcast(FP8X4),
+                            rhs_scale=w_scales[:, g * DOUT : (g + 1) * DOUT],
+                            start=(g == 0), stop=(g == 1),
+                        )
+                nc.vector.tensor_tensor(
+                    out=o_sb[:, r0 : r0 + pair, :], in0=po[:, 0:pair, :], in1=bias2[:, 0:pair, :], op=ALU.add
+                )
+            nc.sync.dma_start(out=out_v[:, row_tile : row_tile + n_rt, :], in_=o_sb[:, 0:n_rt, :])
+            row_tile += n_rt

@@ -19,163 +19,217 @@ DIN = 1024
 DOUT = 256
 ROWS = 8192
 EPS = 2.0 ** -23
-QUARTER = 256
-SUB_ROWS = 32
+PASSES = 2
+PACK = 4
 CHUNKS = [1, 1, 2] + [4] * 14 + [2, 1, 1]
+UNIT = 2
 
 
 def tile_bitlinear_t_kernel(tc, x, weight, bias, gamma, out):
     nc = tc.nc
     assert sum(CHUNKS) * P == ROWS
-    x_q = x.rearrange("b s (a i) -> (b s a) i", a=4).rearrange("(t q) i -> q t i", q=P)
-    out_v = out.flatten_outer_dims().rearrange("(r m) n -> m r n", m=P)
+    x_rows = x.flatten_outer_dims()
+    out_rows = out.flatten_outer_dims()
 
     with ExitStack() as ctx:
         const = ctx.enter_context(tc.tile_pool(name="const", bufs=1))
         xpool = ctx.enter_context(tc.tile_pool(name="xpool", bufs=4))
-        npool = ctx.enter_context(tc.tile_pool(name="npool", bufs=3))
-        gpool = ctx.enter_context(tc.tile_pool(name="gpool", bufs=3))
-        qpool = ctx.enter_context(tc.tile_pool(name="qpool", bufs=3))
-        opool = ctx.enter_context(tc.tile_pool(name="opool", bufs=3))
+        work = ctx.enter_context(tc.tile_pool(name="work", bufs=3))
         small = ctx.enter_context(tc.tile_pool(name="small", bufs=4))
-        ps_t = ctx.enter_context(tc.psum_pool(name="ps_t", bufs=4))
+        ps_t = ctx.enter_context(tc.psum_pool(name="ps_t", bufs=6))
         ps_o = ctx.enter_context(tc.psum_pool(name="ps_o", bufs=2))
-        ps_s = ctx.enter_context(tc.psum_pool(name="ps_s", bufs=2))
-
-        first = CHUNKS[0] * 4
-        xs0 = xpool.tile([P, 16, QUARTER], BF16, name="xs", tag="xs")
-        nc.sync.dma_start(out=xs0[:, 0:first, :], in_=x_q[:, 0:first, :])
-        w_sb = const.tile([P, 2, DIN], BF16)
-        nc.sync.dma_start(out=w_sb[:], in_=weight.rearrange("(h p) k -> p h k", p=P))
-        gam = const.tile([P, QUARTER], BF16)
-        for a in range(4):
-            nc.scalar.dma_start(
-                out=gam[a:P:4, :],
-                in_=gamma[a * QUARTER : (a + 1) * QUARTER].partition_broadcast(SUB_ROWS),
-            )
-        bias_bf = const.tile([P, DOUT], BF16)
-        nc.scalar.dma_start(out=bias_bf[:], in_=bias.partition_broadcast(P))
 
         warm = const.tile([P, 1], F32)
         nc.vector.memset(warm[:], 1.0)
-        nc.scalar.activation(out=warm[:], in_=warm[:], func=ACT.Sqrt)
+        nc.scalar.activation(out=warm[:], in_=warm[:], func=ACT.Abs_reciprocal_sqrt)
+        vec_rows = const.tile([P, P], BF16)
+        nc.vector.memset(vec_rows[:], 0.0)
+        nc.scalar.dma_start(out=vec_rows[0:8, :], in_=gamma.rearrange("(a k) -> a k", k=P))
+        nc.scalar.dma_start(out=vec_rows[8:10, :], in_=bias.rearrange("(a k) -> a k", k=P))
+        w_sb = const.tile([P, 2, DIN], BF16)
         ident = const.tile([P, P], BF16)
         make_identity(nc, ident[:])
-        identf = const.tile([P, P], F32)
-        make_identity(nc, identf[:])
-        grp = const.tile([P, 32], F32)
-        nc.vector.tensor_reduce(
-            out=grp[:], in_=identf[:].rearrange("p (g a) -> p g a", a=4), axis=AX.X, op=ALU.add
-        )
-        same_row = const.tile([P, 32, 4], F32)
-        nc.vector.tensor_copy(out=same_row[:], in_=grp[:].unsqueeze(2).to_broadcast([P, 32, 4]))
+        ident_f32 = const.tile([P, P], F32)
+        nc.vector.tensor_copy(out=ident_f32[:], in_=ident[:])
         ones = const.tile([P, P], F32)
         nc.vector.memset(ones[:], 1.0)
-        bias2 = const.tile([P, 2, DOUT], F32)
-        nc.vector.tensor_copy(out=bias2[:], in_=bias_bf[:].unsqueeze(1).to_broadcast([P, 2, DOUT]))
 
-        w_flat = w_sb[:].rearrange("p h k -> p (h k)")
-        w_abs = const.tile([P, 2 * DIN], BF16)
-        abs_sum = const.tile([P, 1], F32)
-        nc.vector.scalar_tensor_tensor(
-            out=w_abs[:], in0=w_flat, scalar=-1.0, in1=w_flat, op0=ALU.mult, op1=ALU.max,
-            accum_out=abs_sum[:],
+        units = []
+        row_tile = 0
+        for n in CHUNKS:
+            for r in range(0, n, UNIT):
+                units.append({"base": row_tile, "n": n, "r": r, "size": min(UNIT, n - r)})
+            row_tile += n
+        chunk_of = {}
+
+        def load(u):
+            if u["r"] > 0:
+                return
+            xs = xpool.tile([P, 4, DIN], BF16, name="xs", tag="xs")
+            n = u["n"]
+            rows = x_rows[u["base"] * P : (u["base"] + n) * P].rearrange("(p r) k -> p r k", r=n)
+            nc.sync.dma_start(out=xs[:, 0:n, :], in_=rows)
+            chunk_of[u["base"]] = xs
+
+        def stats(u):
+            xs = chunk_of[u["base"]]
+            ssq = small.tile([P, UNIT], F32, name="ssq", tag="ssq")
+            for i in range(u["size"]):
+                sq = small.tile([P, DIN], BF16, name="sq", tag="sq")
+                nc.scalar.activation(
+                    out=sq[:], in_=xs[:, u["r"] + i, :], func=ACT.Square, accum_out=ssq[:, i : i + 1]
+                )
+            rstd = small.tile([P, UNIT], F32, name="rstd", tag="rstd")
+            nc.scalar.activation(
+                out=rstd[:, 0 : u["size"]], in_=ssq[:, 0 : u["size"]], func=ACT.Abs_reciprocal_sqrt,
+                scale=1.0 / DIN, bias=EPS,
+            )
+            u["rstd"] = rstd
+
+        def scale_rows(u):
+            xs = chunk_of[u["base"]]
+            xr = work.tile([P, UNIT, DIN], F32, name="xr", tag="xr")
+            for i in range(u["size"]):
+                nc.gpsimd.tensor_scalar(
+                    out=xr[:, i, :], in0=xs[:, u["r"] + i, :], scalar1=u["rstd"][:, i : i + 1], scalar2=1.0,
+                    op0=ALU.mult, op1=ALU.mult,
+                )
+            u["xr"] = xr
+
+        def turn(u):
+            u["pt"] = []
+            for i in range(u["size"]):
+                for g in range(PASSES):
+                    pt = ps_t.tile([P, PACK, P], F32, name="pt", tag="pt")
+                    for t in range(PACK):
+                        k0 = (g * PACK + t) * P
+                        nc.tensor.transpose(out=pt[:, t, :], in_=u["xr"][:, i, k0 : k0 + P], identity=ident_f32[:])
+                    u["pt"].append(pt)
+
+        def gather(u):
+            grouped = work.tile([P, UNIT, PASSES, P, PACK], BF16, name="grouped", tag="grouped", align_bytes=64)
+            for i in range(u["size"]):
+                for g in range(PASSES):
+                    nc.vector.tensor_tensor(
+                        out=grouped[:, i, g, :, :],
+                        in0=u["pt"][i * PASSES + g][:].rearrange("p t m -> p m t"),
+                        in1=gam[:, g, :].unsqueeze(1).to_broadcast([P, P, PACK]),
+                        op=ALU.mult,
+                    )
+            u["grouped"] = grouped
+
+        def quantise(u):
+            codes = work.tile([P, UNIT * PASSES * P], U32, name="codes", tag="codes", align_bytes=64)
+            scales = work.tile([P, UNIT * PASSES * P], U8, name="scales", tag="scales", align_bytes=64)
+            width = u["size"] * PASSES * P
+            nc.vector.quantize_mx(
+                out=codes[:, 0:width].bitcast(FP8X4), scales=scales[:, 0:width],
+                in_=u["grouped"][:, 0 : u["size"]].rearrange("p i g m t -> p (i g m t)"),
+            )
+            u["codes"], u["scales"] = codes, scales
+
+        def multiply(u):
+            po = ps_o.tile([P, UNIT, DOUT], F32, name="po", tag="po")
+            for i in range(u["size"]):
+                for g in range(PASSES):
+                    cols = slice((i * PASSES + g) * P, (i * PASSES + g + 1) * P)
+                    nc.tensor.matmul_mx(
+                        out=po[:, i, :],
+                        lhsT=u["codes"][:, cols].bitcast(FP8X4), lhsT_scale=u["scales"][:, cols],
+                        rhs=w_codes[:, g * DOUT : (g + 1) * DOUT].bitcast(FP8X4),
+                        rhs_scale=w_scales[:, g * DOUT : (g + 1) * DOUT],
+                        start=(g == 0), stop=(g == PASSES - 1),
+                    )
+            u["po"] = po
+
+        def finish(u):
+            size = u["size"]
+            o_sb = work.tile([P, UNIT, DOUT], F32, name="o_sb", tag="o_sb")
+            nc.vector.tensor_tensor(
+                out=o_sb[:, 0:size, :], in0=u["po"][:, 0:size, :], in1=bias2[:, 0:size, :], op=ALU.add
+            )
+            n = u["n"]
+            rows = out_rows[u["base"] * P : (u["base"] + n) * P].rearrange("(p r) c -> p r c", r=n)
+            nc.sync.dma_start(out=rows[:, u["r"] : u["r"] + size, :], in_=o_sb[:, 0:size, :])
+
+        for u in units[0:2]:
+            load(u)
+        nc.sync.dma_start(out=w_sb[:], in_=weight.rearrange("(h p) k -> p h k", p=P))
+        for u in units[2:4]:
+            load(u)
+        stats(units[0])
+
+        vec_ps = ps_t.tile([P, P], BF16, name="vec_ps", tag="pt")
+        nc.tensor.transpose(out=vec_ps[:], in_=vec_rows[:], identity=ident[:])
+        gam = const.tile([P, PASSES, PACK], F32)
+        nc.vector.tensor_copy(out=gam[:].rearrange("p g t -> p (g t)"), in_=vec_ps[:, 0:8])
+        bias_t = const.tile([P, 2, P], F32)
+        nc.vector.tensor_copy(out=bias_t[:], in_=vec_ps[:, 8:10].unsqueeze(2).to_broadcast([P, 2, P]))
+        bias_ps = ps_o.tile([P, UNIT, DOUT], F32, name="bias_ps", tag="po")
+        for i in range(UNIT):
+            for h in range(2):
+                nc.tensor.transpose(
+                    out=bias_ps[:, i, h * P : (h + 1) * P], in_=bias_t[:, h, :], identity=ident_f32[:]
+                )
+        bias2 = const.tile([P, UNIT, DOUT], F32)
+        nc.vector.tensor_copy(out=bias2[:], in_=bias_ps[:])
+
+        abs_sum = const.tile([P, 2], F32)
+        w_abs = const.tile([P, DIN], BF16)
+        nc.vector.tensor_reduce(
+            out=abs_sum[:, 0:1], in_=w_sb[:, 0, :], axis=AX.X, op=ALU.add, apply_absolute_value=True
         )
-        tot = ps_s.tile([P, 1], F32, tag="ps")
+        nc.vector.tensor_reduce(
+            out=abs_sum[:, 1:2], in_=w_sb[:, 1, :], axis=AX.X, op=ALU.add, apply_absolute_value=True
+        )
+        tot = ps_o.tile([P, 2], F32, name="tot", tag="po")
         nc.tensor.matmul(tot[:], lhsT=ones[:], rhs=abs_sum[:], start=True, stop=True)
+        total = const.tile([P, 1], F32)
+        nc.vector.tensor_reduce(out=total[:], in_=tot[:], axis=AX.X, op=ALU.add)
         thr = const.tile([P, 1], F32)
-        nc.vector.tensor_scalar(out=thr[:], in0=tot[:], scalar1=1.0 / (DOUT * DIN), scalar2=None, op0=ALU.mult)
+        nc.vector.tensor_scalar(out=thr[:], in0=total[:], scalar1=1.0 / (DOUT * DIN), scalar2=None, op0=ALU.mult)
         nthr = const.tile([P, 1], F32)
-        nc.vector.tensor_scalar(out=nthr[:], in0=tot[:], scalar1=-1.0 / (DOUT * DIN), scalar2=None, op0=ALU.mult)
+        nc.vector.tensor_scalar(out=nthr[:], in0=total[:], scalar1=-1.0 / (DOUT * DIN), scalar2=None, op0=ALU.mult)
+        w_flat = w_sb[:].rearrange("p h k -> p (h k)")
+        w_pos = const.tile([P, 2 * DIN], BF16)
+        nc.vector.tensor_scalar(out=w_pos[:], in0=w_flat, scalar1=thr[:, 0:1], scalar2=None, op0=ALU.is_gt)
         w_neg = const.tile([P, 2 * DIN], BF16)
         nc.vector.tensor_scalar(out=w_neg[:], in0=w_flat, scalar1=nthr[:, 0:1], scalar2=None, op0=ALU.is_lt)
         w_t = const.tile([P, 2, DIN], BF16)
-        nc.vector.scalar_tensor_tensor(
-            out=w_t[:].rearrange("p h k -> p (h k)"), in0=w_flat, scalar=thr[:, 0:1], in1=w_neg[:],
-            op0=ALU.is_gt, op1=ALU.subtract,
+        nc.vector.tensor_tensor(
+            out=w_t[:].rearrange("p h k -> p (h k)"), in0=w_pos[:], in1=w_neg[:], op=ALU.subtract
         )
-        w_grouped = const.tile([P, 2, DOUT, 4], BF16, align_bytes=64)
+        w_grouped = const.tile([P, PASSES, DOUT, PACK], BF16, align_bytes=64)
         for h in range(2):
-            w_ps = ps_t.tile([P, 8, P], BF16, tag="pt")
-            for kb in range(8):
-                nc.tensor.transpose(out=w_ps[:, kb, :], in_=w_t[:, h, kb * P : (kb + 1) * P], identity=ident[:])
-            for g in range(2):
+            w_ps = ps_t.tile([P, PASSES, PACK, P], BF16, name="w_ps", tag="pt")
+            for g in range(PASSES):
+                for t in range(PACK):
+                    k0 = (g * PACK + t) * P
+                    nc.tensor.transpose(out=w_ps[:, g, t, :], in_=w_t[:, h, k0 : k0 + P], identity=ident[:])
+            for g in range(PASSES):
                 nc.vector.tensor_copy(
-                    out=w_grouped[:, g, h * P : (h + 1) * P, :].rearrange("c n (b a) -> c n b a", b=2),
-                    in_=w_ps[:, 4 * g : 4 * g + 4, :].rearrange("c (a b) n -> c n b a", a=2),
+                    out=w_grouped[:, g, h * P : (h + 1) * P, :], in_=w_ps[:, g].rearrange("p t n -> p n t")
                 )
-        w_codes = const.tile([P, 2 * DOUT], U32, align_bytes=64)
-        w_scales = const.tile([P, 2 * DOUT], U8, align_bytes=64)
+        w_codes = const.tile([P, PASSES * DOUT], U32, align_bytes=64)
+        w_scales = const.tile([P, PASSES * DOUT], U8, align_bytes=64)
         nc.vector.quantize_mx(
             out=w_codes[:].bitcast(FP8X4), scales=w_scales[:],
-            in_=w_grouped[:].rearrange("c g n j -> c (g n j)"),
+            in_=w_grouped[:].rearrange("p g n t -> p (g n t)"),
         )
 
-        row_tile = 0
-        for ci, n_rt in enumerate(CHUNKS):
-            n_sub = 4 * n_rt
-            t0 = 4 * row_tile
-            if ci == 0:
-                xs = xs0
-            else:
-                xs = xpool.tile([P, 16, QUARTER], BF16, name="xs", tag="xs")
-                nc.sync.dma_start(out=xs[:, 0:n_sub, :], in_=x_q[:, t0 : t0 + n_sub, :])
-            ssq = small.tile([P, 16], F32)
-            for t in range(n_sub):
-                sq = small.tile([P, QUARTER], BF16)
-                nc.scalar.activation(out=sq[:], in_=xs[:, t, :], func=ACT.Square, accum_out=ssq[:, t : t + 1])
-            ms = ps_s.tile([P, 16], F32, tag="ps")
-            nc.tensor.matmul(
-                ms[:, 0:n_sub], lhsT=same_row[:].rearrange("p g a -> p (g a)"), rhs=ssq[:, 0:n_sub],
-                start=True, stop=True,
-            )
-            std = small.tile([P, 16], F32)
-            nc.scalar.activation(out=std[:, 0:n_sub], in_=ms[:, 0:n_sub], func=ACT.Sqrt, scale=1.0 / DIN, bias=EPS)
-            rstd = small.tile([P, 16], F32)
-            nc.vector.reciprocal(out=rstd[:, 0:n_sub], in_=std[:, 0:n_sub])
-            xn = npool.tile([P, 16, QUARTER], BF16)
-            for t in range(n_sub):
-                nc.vector.scalar_tensor_tensor(
-                    out=xn[:, t, :], in0=xs[:, t, :], scalar=rstd[:, t : t + 1], in1=gam[:],
-                    op0=ALU.mult, op1=ALU.mult,
-                )
-            grouped = gpool.tile([P, 4, 2, P, 4], BF16, align_bytes=64)
-            for r in range(n_rt):
-                pt = ps_t.tile([P, 2, P, 4], BF16, tag="pt")
-                for s in range(4):
-                    for b in range(2):
-                        nc.tensor.transpose(
-                            out=pt[:, :, 32 * s : 32 * s + 32, 2 * b : 2 * b + 2].rearrange("c g w a -> c w g a"),
-                            in_=xn[:, 4 * r + s, b * P : (b + 1) * P],
-                            identity=ident[:],
-                        )
-                nc.scalar.copy(
-                    out=grouped[:, r].rearrange("c g m j -> c (g m j)"),
-                    in_=pt[:].rearrange("c g m j -> c (g m j)"),
-                )
-            codes = qpool.tile([P, 4 * 2 * P], U32, align_bytes=64)
-            scales = qpool.tile([P, 4 * 2 * P], U8, align_bytes=64)
-            width = n_rt * 2 * P
-            nc.vector.quantize_mx(
-                out=codes[:, 0:width].bitcast(FP8X4), scales=scales[:, 0:width],
-                in_=grouped[:, 0:n_rt].rearrange("c r g m j -> c (r g m j)"),
-            )
-            o_sb = opool.tile([P, 4, DOUT], F32)
-            for r0 in range(0, n_rt, 2):
-                pair = min(2, n_rt - r0)
-                po = ps_o.tile([P, 2, DOUT], F32)
-                for r in range(r0, r0 + pair):
-                    for g in range(2):
-                        cols = slice((2 * r + g) * P, (2 * r + g + 1) * P)
-                        nc.tensor.matmul_mx(
-                            out=po[:, r - r0, :],
-                            lhsT=codes[:, cols].bitcast(FP8X4), lhsT_scale=scales[:, cols],
-                            rhs=w_codes[:, g * DOUT : (g + 1) * DOUT].bitcast(FP8X4),
-                            rhs_scale=w_scales[:, g * DOUT : (g + 1) * DOUT],
-                            start=(g == 0), stop=(g == 1),
-                        )
-                nc.vector.tensor_tensor(
-                    out=o_sb[:, r0 : r0 + pair, :], in0=po[:, 0:pair, :], in1=bias2[:, 0:pair, :], op=ALU.add
-                )
-            nc.sync.dma_start(out=out_v[:, row_tile : row_tile + n_rt, :], in_=o_sb[:, 0:n_rt, :])
-            row_tile += n_rt
+        n_units = len(units)
+        for s in range(n_units + 4):
+            if 4 <= s + 3 < n_units:
+                load(units[s + 3])
+            if 1 <= s < n_units:
+                stats(units[s])
+            if s < n_units:
+                scale_rows(units[s])
+            if 0 <= s - 1 < n_units:
+                turn(units[s - 1])
+                gather(units[s - 1])
+            if 0 <= s - 2 < n_units:
+                quantise(units[s - 2])
+            if 0 <= s - 3 < n_units:
+                multiply(units[s - 3])
+                finish(units[s - 3])

@@ -36,19 +36,23 @@ def tile_bitlinear_t_kernel(tc, x, weight, bias, gamma, out):
         xpool = ctx.enter_context(tc.tile_pool(name="xpool", bufs=4))
         work = ctx.enter_context(tc.tile_pool(name="work", bufs=3))
         small = ctx.enter_context(tc.tile_pool(name="small", bufs=4))
-        ps_t = ctx.enter_context(tc.psum_pool(name="ps_t", bufs=6))
-        ps_o = ctx.enter_context(tc.psum_pool(name="ps_o", bufs=2))
+        ps_t = ctx.enter_context(tc.psum_pool(name="ps_t", bufs=5))
+        ps_o = ctx.enter_context(tc.psum_pool(name="ps_o", bufs=3))
+
+        ctx.enter_context(tc.manual_schedule())
 
         warm = const.tile([P, 1], F32)
         nc.vector.memset(warm[:], 1.0)
         nc.scalar.activation(out=warm[:], in_=warm[:], func=ACT.Abs_reciprocal_sqrt)
         vec_rows = const.tile([P, P], BF16)
         nc.vector.memset(vec_rows[:], 0.0)
-        nc.scalar.dma_start(out=vec_rows[0:8, :], in_=gamma.rearrange("(a k) -> a k", k=P))
-        nc.scalar.dma_start(out=vec_rows[8:10, :], in_=bias.rearrange("(a k) -> a k", k=P))
+        nc.sync.dma_start(out=vec_rows[0:8, :], in_=gamma.rearrange("(a k) -> a k", k=P))
+        nc.sync.dma_start(out=vec_rows[8:10, :], in_=bias.rearrange("(a k) -> a k", k=P))
         w_sb = const.tile([P, 2, DIN], BF16)
         ident = const.tile([P, P], BF16)
         make_identity(nc, ident[:])
+        neg_ident = const.tile([P, P], BF16)
+        nc.vector.tensor_scalar(out=neg_ident[:], in0=ident[:], scalar1=-1.0, scalar2=None, op0=ALU.mult)
         ident_f32 = const.tile([P, P], F32)
         nc.vector.tensor_copy(out=ident_f32[:], in_=ident[:])
         ones = const.tile([P, P], F32)
@@ -58,7 +62,10 @@ def tile_bitlinear_t_kernel(tc, x, weight, bias, gamma, out):
         row_tile = 0
         for n in CHUNKS:
             for r in range(0, n, UNIT):
-                units.append({"base": row_tile, "n": n, "r": r, "size": min(UNIT, n - r)})
+                units.append({
+                    "base": row_tile, "n": n, "r": r, "size": min(UNIT, n - r),
+                    "channels_first": len(units) % 3 > 0,
+                })
             row_tile += n
         chunk_of = {}
 
@@ -71,20 +78,22 @@ def tile_bitlinear_t_kernel(tc, x, weight, bias, gamma, out):
             nc.sync.dma_start(out=xs[:, 0:n, :], in_=rows)
             chunk_of[u["base"]] = xs
 
-        def stats(u):
-            xs = chunk_of[u["base"]]
-            ssq = small.tile([P, UNIT], F32, name="ssq", tag="ssq")
-            for i in range(u["size"]):
+        def square(u, i):
+            if i == 0:
+                u["ssq"] = small.tile([P, UNIT], F32, name="ssq", tag="ssq")
+            if i < u["size"]:
                 sq = small.tile([P, DIN], BF16, name="sq", tag="sq")
                 nc.scalar.activation(
-                    out=sq[:], in_=xs[:, u["r"] + i, :], func=ACT.Square, accum_out=ssq[:, i : i + 1]
+                    out=sq[:], in_=chunk_of[u["base"]][:, u["r"] + i, :], func=ACT.Square,
+                    accum_out=u["ssq"][:, i : i + 1],
                 )
-            rstd = small.tile([P, UNIT], F32, name="rstd", tag="rstd")
+
+        def root(u):
+            u["rstd"] = small.tile([P, UNIT], F32, name="rstd", tag="rstd")
             nc.scalar.activation(
-                out=rstd[:, 0 : u["size"]], in_=ssq[:, 0 : u["size"]], func=ACT.Abs_reciprocal_sqrt,
+                out=u["rstd"][:, 0 : u["size"]], in_=u["ssq"][:, 0 : u["size"]], func=ACT.Abs_reciprocal_sqrt,
                 scale=1.0 / DIN, bias=EPS,
             )
-            u["rstd"] = rstd
 
         def scale_rows(u):
             xs = chunk_of[u["base"]]
@@ -106,17 +115,20 @@ def tile_bitlinear_t_kernel(tc, x, weight, bias, gamma, out):
                         nc.tensor.transpose(out=pt[:, t, :], in_=u["xr"][:, i, k0 : k0 + P], identity=ident_f32[:])
                     u["pt"].append(pt)
 
-        def gather(u):
-            grouped = work.tile([P, UNIT, PASSES, P, PACK], BF16, name="grouped", tag="grouped", align_bytes=64)
-            for i in range(u["size"]):
-                for g in range(PASSES):
-                    nc.vector.tensor_tensor(
-                        out=grouped[:, i, g, :, :],
-                        in0=u["pt"][i * PASSES + g][:].rearrange("p t m -> p m t"),
-                        in1=gam[:, g, :].unsqueeze(1).to_broadcast([P, P, PACK]),
-                        op=ALU.mult,
-                    )
-            u["grouped"] = grouped
+        def gather(u, b):
+            size = u["size"]
+            if b == 0:
+                u["grouped"] = work.tile([P, UNIT * DIN], BF16, name="grouped", tag="grouped", align_bytes=64)
+            if b < size * PASSES:
+                grouped = u["grouped"][:, 0 : size * DIN].rearrange(
+                    "p (g i m t) -> p g i m t", g=PASSES, i=size, t=PACK
+                )
+                nc.vector.tensor_tensor(
+                    out=grouped[:, b % PASSES, b // PASSES, :, :],
+                    in0=u["pt"][b][:].rearrange("p t m -> p m t"),
+                    in1=gam[:, b % PASSES, :].unsqueeze(1).to_broadcast([P, P, PACK]),
+                    op=ALU.mult,
+                )
 
         def quantise(u):
             codes = work.tile([P, UNIT * PASSES * P], U32, name="codes", tag="codes", align_bytes=64)
@@ -124,45 +136,88 @@ def tile_bitlinear_t_kernel(tc, x, weight, bias, gamma, out):
             width = u["size"] * PASSES * P
             nc.vector.quantize_mx(
                 out=codes[:, 0:width].bitcast(FP8X4), scales=scales[:, 0:width],
-                in_=u["grouped"][:, 0 : u["size"]].rearrange("p i g m t -> p (i g m t)"),
+                in_=u["grouped"][:, 0 : width * PACK],
             )
             u["codes"], u["scales"] = codes, scales
 
         def multiply(u):
-            po = ps_o.tile([P, UNIT, DOUT], F32, name="po", tag="po")
-            for i in range(u["size"]):
-                for g in range(PASSES):
-                    cols = slice((i * PASSES + g) * P, (i * PASSES + g + 1) * P)
-                    nc.tensor.matmul_mx(
-                        out=po[:, i, :],
-                        lhsT=u["codes"][:, cols].bitcast(FP8X4), lhsT_scale=u["scales"][:, cols],
-                        rhs=w_codes[:, g * DOUT : (g + 1) * DOUT].bitcast(FP8X4),
-                        rhs_scale=w_scales[:, g * DOUT : (g + 1) * DOUT],
-                        start=(g == 0), stop=(g == PASSES - 1),
+            size = u["size"]
+            po = ps_o.tile([P, UNIT * DOUT], F32, name="po", tag="po")
+            if u["channels_first"]:
+                for h in range(2):
+                    for g in range(PASSES):
+                        ch = slice(g * DOUT + h * P, g * DOUT + (h + 1) * P)
+                        rows = slice(g * size * P, (g + 1) * size * P)
+                        nc.tensor.matmul_mx(
+                            out=po[:, h * size * P : (h + 1) * size * P],
+                            lhsT=w_codes[:, ch].bitcast(FP8X4), lhsT_scale=w_scales[:, ch],
+                            rhs=u["codes"][:, rows].bitcast(FP8X4), rhs_scale=u["scales"][:, rows],
+                            start=(g == 0), stop=(g == PASSES - 1),
+                        )
+            else:
+                for i in range(size):
+                    for g in range(PASSES):
+                        rows = slice((g * size + i) * P, (g * size + i + 1) * P)
+                        ch = slice(g * DOUT, (g + 1) * DOUT)
+                        nc.tensor.matmul_mx(
+                            out=po[:, i * DOUT : (i + 1) * DOUT],
+                            lhsT=u["codes"][:, rows].bitcast(FP8X4), lhsT_scale=u["scales"][:, rows],
+                            rhs=w_codes[:, ch].bitcast(FP8X4), rhs_scale=w_scales[:, ch],
+                            start=(g == 0), stop=(g == PASSES - 1),
+                        )
+            u["po"] = po
+
+        def add_bias(u):
+            size = u["size"]
+            o_sb = work.tile([P, UNIT * DOUT], F32, name="o_sb", tag="o_sb")
+            if u["channels_first"]:
+                for h in range(2):
+                    cols = slice(h * size * P, (h + 1) * size * P)
+                    nc.scalar.activation(
+                        out=o_sb[:, cols], in_=u["po"][:, cols], func=ACT.Identity, bias=bias_col[:, h : h + 1]
+                    )
+            else:
+                cols = slice(0, size * DOUT)
+                nc.vector.tensor_tensor(out=o_sb[:, cols], in0=u["po"][:, cols], in1=bias2[:, cols], op=ALU.add)
+            u["o_sb"] = o_sb
+
+        def turn_back(u):
+            po = ps_o.tile([P, UNIT * DOUT], F32, name="po", tag="po")
+            for h in range(2):
+                for i in range(u["size"]):
+                    nc.tensor.transpose(
+                        out=po[:, i * DOUT + h * P : i * DOUT + (h + 1) * P],
+                        in_=u["o_sb"][:, (h * u["size"] + i) * P : (h * u["size"] + i + 1) * P],
+                        identity=ident_f32[:],
                     )
             u["po"] = po
 
-        def finish(u):
+        def copy_out(u):
+            cols = slice(0, u["size"] * DOUT)
+            o_rows = work.tile([P, UNIT * DOUT], F32, name="o_rows", tag="o_rows")
+            nc.scalar.copy(out=o_rows[:, cols], in_=u["po"][:, cols])
+            u["o_sb"] = o_rows
+
+        def store(u):
             size = u["size"]
-            o_sb = work.tile([P, UNIT, DOUT], F32, name="o_sb", tag="o_sb")
-            nc.vector.tensor_tensor(
-                out=o_sb[:, 0:size, :], in0=u["po"][:, 0:size, :], in1=bias2[:, 0:size, :], op=ALU.add
-            )
             n = u["n"]
             rows = out_rows[u["base"] * P : (u["base"] + n) * P].rearrange("(p r) c -> p r c", r=n)
-            nc.sync.dma_start(out=rows[:, u["r"] : u["r"] + size, :], in_=o_sb[:, 0:size, :])
+            nc.sync.dma_start(
+                out=rows[:, u["r"] : u["r"] + size, :],
+                in_=u["o_sb"][:, 0 : size * DOUT].rearrange("p (i c) -> p i c", i=size),
+            )
 
-        for u in units[0:2]:
-            load(u)
+        load(units[0])
         nc.sync.dma_start(out=w_sb[:], in_=weight.rearrange("(h p) k -> p h k", p=P))
-        for u in units[2:4]:
+        for u in units[1:4]:
             load(u)
-        stats(units[0])
 
         vec_ps = ps_t.tile([P, P], BF16, name="vec_ps", tag="pt")
         nc.tensor.transpose(out=vec_ps[:], in_=vec_rows[:], identity=ident[:])
         gam = const.tile([P, PASSES, PACK], F32)
         nc.vector.tensor_copy(out=gam[:].rearrange("p g t -> p (g t)"), in_=vec_ps[:, 0:8])
+        bias_col = const.tile([P, 2], F32)
+        nc.vector.tensor_copy(out=bias_col[:], in_=vec_ps[:, 8:10])
         bias_t = const.tile([P, 2, P], F32)
         nc.vector.tensor_copy(out=bias_t[:], in_=vec_ps[:, 8:10].unsqueeze(2).to_broadcast([P, 2, P]))
         bias_ps = ps_o.tile([P, UNIT, DOUT], F32, name="bias_ps", tag="po")
@@ -171,17 +226,12 @@ def tile_bitlinear_t_kernel(tc, x, weight, bias, gamma, out):
                 nc.tensor.transpose(
                     out=bias_ps[:, i, h * P : (h + 1) * P], in_=bias_t[:, h, :], identity=ident_f32[:]
                 )
-        bias2 = const.tile([P, UNIT, DOUT], F32)
-        nc.vector.tensor_copy(out=bias2[:], in_=bias_ps[:])
 
         abs_sum = const.tile([P, 2], F32)
-        w_abs = const.tile([P, DIN], BF16)
-        nc.vector.tensor_reduce(
-            out=abs_sum[:, 0:1], in_=w_sb[:, 0, :], axis=AX.X, op=ALU.add, apply_absolute_value=True
-        )
-        nc.vector.tensor_reduce(
-            out=abs_sum[:, 1:2], in_=w_sb[:, 1, :], axis=AX.X, op=ALU.add, apply_absolute_value=True
-        )
+        for h in range(2):
+            nc.vector.tensor_reduce(
+                out=abs_sum[:, h : h + 1], in_=w_sb[:, h, :], axis=AX.X, op=ALU.add, apply_absolute_value=True
+            )
         tot = ps_o.tile([P, 2], F32, name="tot", tag="po")
         nc.tensor.matmul(tot[:], lhsT=ones[:], rhs=abs_sum[:], start=True, stop=True)
         total = const.tile([P, 1], F32)
@@ -191,45 +241,78 @@ def tile_bitlinear_t_kernel(tc, x, weight, bias, gamma, out):
         nthr = const.tile([P, 1], F32)
         nc.vector.tensor_scalar(out=nthr[:], in0=total[:], scalar1=-1.0 / (DOUT * DIN), scalar2=None, op0=ALU.mult)
         w_flat = w_sb[:].rearrange("p h k -> p (h k)")
-        w_pos = const.tile([P, 2 * DIN], BF16)
-        nc.vector.tensor_scalar(out=w_pos[:], in0=w_flat, scalar1=thr[:, 0:1], scalar2=None, op0=ALU.is_gt)
-        w_neg = const.tile([P, 2 * DIN], BF16)
-        nc.vector.tensor_scalar(out=w_neg[:], in0=w_flat, scalar1=nthr[:, 0:1], scalar2=None, op0=ALU.is_lt)
-        w_t = const.tile([P, 2, DIN], BF16)
-        nc.vector.tensor_tensor(
-            out=w_t[:].rearrange("p h k -> p (h k)"), in0=w_pos[:], in1=w_neg[:], op=ALU.subtract
+        w_pos = const.tile([P, 2, DIN], BF16)
+        nc.vector.tensor_scalar(
+            out=w_pos[:].rearrange("p h k -> p (h k)"), in0=w_flat, scalar1=thr[:, 0:1], scalar2=None, op0=ALU.is_gt
+        )
+        w_neg = const.tile([P, 2, DIN], BF16)
+        nc.vector.tensor_scalar(
+            out=w_neg[:].rearrange("p h k -> p (h k)"), in0=w_flat, scalar1=nthr[:, 0:1], scalar2=None, op0=ALU.is_lt
         )
         w_grouped = const.tile([P, PASSES, DOUT, PACK], BF16, align_bytes=64)
-        for h in range(2):
-            w_ps = ps_t.tile([P, PASSES, PACK, P], BF16, name="w_ps", tag="pt")
-            for g in range(PASSES):
-                for t in range(PACK):
-                    k0 = (g * PACK + t) * P
-                    nc.tensor.transpose(out=w_ps[:, g, t, :], in_=w_t[:, h, k0 : k0 + P], identity=ident[:])
-            for g in range(PASSES):
-                nc.vector.tensor_copy(
-                    out=w_grouped[:, g, h * P : (h + 1) * P, :], in_=w_ps[:, g].rearrange("p t n -> p n t")
-                )
         w_codes = const.tile([P, PASSES * DOUT], U32, align_bytes=64)
         w_scales = const.tile([P, PASSES * DOUT], U8, align_bytes=64)
-        nc.vector.quantize_mx(
-            out=w_codes[:].bitcast(FP8X4), scales=w_scales[:],
-            in_=w_grouped[:].rearrange("p g n t -> p (g n t)"),
-        )
 
-        n_units = len(units)
-        for s in range(n_units + 4):
-            if 4 <= s + 3 < n_units:
-                load(units[s + 3])
-            if 1 <= s < n_units:
-                stats(units[s])
-            if s < n_units:
-                scale_rows(units[s])
-            if 0 <= s - 1 < n_units:
-                turn(units[s - 1])
-                gather(units[s - 1])
-            if 0 <= s - 2 < n_units:
-                quantise(units[s - 2])
-            if 0 <= s - 3 < n_units:
-                multiply(units[s - 3])
-                finish(units[s - 3])
+        def turn_weights():
+            for h in range(2):
+                for g in range(PASSES):
+                    w_ps = ps_t.tile([P, PACK, P], F32, name="w_ps", tag="pt")
+                    for t in range(PACK):
+                        k_cols = slice((g * PACK + t) * P, (g * PACK + t + 1) * P)
+                        nc.tensor.matmul(w_ps[:, t, :], lhsT=w_pos[:, h, k_cols], rhs=ident[:], start=True, stop=False)
+                        nc.tensor.matmul(w_ps[:, t, :], lhsT=w_neg[:, h, k_cols], rhs=neg_ident[:], start=False, stop=True)
+                    nc.scalar.copy(
+                        out=w_grouped[:, g, h * P : (h + 1) * P, :], in_=w_ps[:].rearrange("p t n -> p n t")
+                    )
+
+        def quantise_weights():
+            nc.vector.quantize_mx(
+                out=w_codes[:].bitcast(FP8X4), scales=w_scales[:],
+                in_=w_grouped[:].rearrange("p g n t -> p (g n t)"),
+            )
+
+        bias2 = const.tile([P, UNIT * DOUT], F32)
+        nc.vector.tensor_copy(out=bias2[:], in_=bias_ps[:].rearrange("p i c -> p (i c)"))
+
+        def at(i):
+            return units[i] if 0 <= i < len(units) else None
+
+        for s in range(len(units) + 8):
+            new, scale, now, quant, mult, bias_u, back, last = [at(s - d) for d in range(8)]
+            if new:
+                square(new, 0)
+            if bias_u and bias_u["channels_first"]:
+                add_bias(bias_u)
+            if new:
+                square(new, 1)
+                root(new)
+            if last and last["channels_first"]:
+                copy_out(last)
+            if scale:
+                scale_rows(scale)
+            if now:
+                turn(now)
+                gather(now, 0)
+            if quant:
+                quantise(quant)
+            if s == 4:
+                quantise_weights()
+            if now:
+                gather(now, 1)
+                gather(now, 2)
+            if bias_u and not bias_u["channels_first"]:
+                add_bias(bias_u)
+            if now:
+                gather(now, 3)
+            if back and back["channels_first"]:
+                turn_back(back)
+            if s == 3:
+                turn_weights()
+            if mult:
+                multiply(mult)
+            if bias_u and not bias_u["channels_first"]:
+                store(bias_u)
+            if last and last["channels_first"]:
+                store(last)
+            if s >= 1 and at(s + 3):
+                load(at(s + 3))

@@ -22,6 +22,7 @@ EPS = 2.0 ** -23
 PASSES = 2
 PACK = 4
 CHUNKS = [1, 1, 2] + [4] * 14 + [2, 1, 1]
+G_COLS = 512
 UNIT = 2
 
 
@@ -99,10 +100,11 @@ def tile_bitlinear_t_kernel(tc, x, weight, bias, gamma, out):
             xs = chunk_of[u["base"]]
             xr = work.tile([P, UNIT, DIN], F32, name="xr", tag="xr")
             for i in range(u["size"]):
-                nc.gpsimd.tensor_scalar(
-                    out=xr[:, i, :], in0=xs[:, u["r"] + i, :], scalar1=u["rstd"][:, i : i + 1], scalar2=1.0,
-                    op0=ALU.mult, op1=ALU.mult,
-                )
+                for k0 in range(0, DIN, G_COLS):
+                    nc.gpsimd.tensor_scalar(
+                        out=xr[:, i, k0 : k0 + G_COLS], in0=xs[:, u["r"] + i, k0 : k0 + G_COLS],
+                        scalar1=u["rstd"][:, i : i + 1], scalar2=1.0, op0=ALU.mult, op1=ALU.mult,
+                    )
             u["xr"] = xr
 
         def turn(u):

@@ -22,8 +22,9 @@ EPS = 2.0 ** -23
 PASSES = 2
 PACK = 4
 CHUNKS = [1, 1, 2] + [4] * 14 + [2, 1, 1]
-G_COLS = 512
 UNIT = 2
+GPSIMD_EVERY = 3
+VECTOR_COPY_EVERY = 4
 
 
 def tile_bitlinear_t_kernel(tc, x, weight, bias, gamma, out):
@@ -35,9 +36,11 @@ def tile_bitlinear_t_kernel(tc, x, weight, bias, gamma, out):
     with ExitStack() as ctx:
         const = ctx.enter_context(tc.tile_pool(name="const", bufs=1))
         xpool = ctx.enter_context(tc.tile_pool(name="xpool", bufs=4))
+        npool = ctx.enter_context(tc.tile_pool(name="npool", bufs=4))
         work = ctx.enter_context(tc.tile_pool(name="work", bufs=3))
         small = ctx.enter_context(tc.tile_pool(name="small", bufs=4))
-        ps_t = ctx.enter_context(tc.psum_pool(name="ps_t", bufs=5))
+        ps_t = ctx.enter_context(tc.psum_pool(name="ps_t", bufs=4))
+        ps_g = ctx.enter_context(tc.psum_pool(name="ps_g", bufs=1))
         ps_o = ctx.enter_context(tc.psum_pool(name="ps_o", bufs=3))
 
         ctx.enter_context(tc.manual_schedule())
@@ -47,8 +50,6 @@ def tile_bitlinear_t_kernel(tc, x, weight, bias, gamma, out):
         nc.scalar.activation(out=warm[:], in_=warm[:], func=ACT.Abs_reciprocal_sqrt)
         vec_rows = const.tile([P, P], BF16)
         nc.vector.memset(vec_rows[:], 0.0)
-        nc.sync.dma_start(out=vec_rows[0:8, :], in_=gamma.rearrange("(a k) -> a k", k=P))
-        nc.sync.dma_start(out=vec_rows[8:10, :], in_=bias.rearrange("(a k) -> a k", k=P))
         w_sb = const.tile([P, 2, DIN], BF16)
         ident = const.tile([P, P], BF16)
         make_identity(nc, ident[:])
@@ -65,7 +66,6 @@ def tile_bitlinear_t_kernel(tc, x, weight, bias, gamma, out):
             for r in range(0, n, UNIT):
                 units.append({
                     "base": row_tile, "n": n, "r": r, "size": min(UNIT, n - r),
-                    "channels_first": len(units) % 3 > 0,
                 })
             row_tile += n
         chunk_of = {}
@@ -96,40 +96,62 @@ def tile_bitlinear_t_kernel(tc, x, weight, bias, gamma, out):
                 scale=1.0 / DIN, bias=EPS,
             )
 
-        def scale_rows(u):
-            xs = chunk_of[u["base"]]
-            xr = work.tile([P, UNIT, DIN], F32, name="xr", tag="xr")
-            for i in range(u["size"]):
-                for k0 in range(0, DIN, G_COLS):
-                    nc.gpsimd.tensor_scalar(
-                        out=xr[:, i, k0 : k0 + G_COLS], in0=xs[:, u["r"] + i, k0 : k0 + G_COLS],
-                        scalar1=u["rstd"][:, i : i + 1], scalar2=1.0, op0=ALU.mult, op1=ALU.mult,
+        def tiles(u):
+            return range(u["size"])
+
+        def on_gpsimd(u, i):
+            return (u["base"] + u["r"] + i) % GPSIMD_EVERY == GPSIMD_EVERY - 1
+
+        def on_vector(u, i):
+            return (u["base"] + u["r"] + i) % VECTOR_COPY_EVERY == VECTOR_COPY_EVERY - 1
+
+        def times_gamma(u):
+            u["xn"] = npool.tile([P, UNIT, DIN], BF16, name="xn", tag="xn")
+            for i in tiles(u):
+                if on_gpsimd(u, i):
+                    u["xg"] = work.tile([P, DIN], F32, name="xg", tag="xg")
+                    nc.gpsimd.tensor_tensor(
+                        out=u["xg"][:], in0=chunk_of[u["base"]][:, u["r"] + i, :], in1=gam_rows[:], op=ALU.mult
                     )
-            u["xr"] = xr
+
+        def times_rstd(u):
+            for i in tiles(u):
+                if on_gpsimd(u, i):
+                    nc.gpsimd.tensor_scalar(
+                        out=u["xn"][:, i, :], in0=u["xg"][:], scalar1=u["rstd"][:, i : i + 1], scalar2=1.0,
+                        op0=ALU.mult, op1=ALU.mult,
+                    )
+
+        def normalise(u, i):
+            if i < u["size"] and not on_gpsimd(u, i):
+                nc.vector.scalar_tensor_tensor(
+                    out=u["xn"][:, i, :], in0=chunk_of[u["base"]][:, u["r"] + i, :],
+                    scalar=u["rstd"][:, i : i + 1], in1=gam_ps[:], op0=ALU.mult, op1=ALU.mult,
+                )
 
         def turn(u):
             u["pt"] = []
-            for i in range(u["size"]):
+            for i in tiles(u):
+                words = u["xn"][:, i, :].bitcast(F32)
+                pt = ps_t.tile([P, PASSES, 2, P], F32, name="pt", tag="pt")
                 for g in range(PASSES):
-                    pt = ps_t.tile([P, PACK, P], F32, name="pt", tag="pt")
-                    for t in range(PACK):
-                        k0 = (g * PACK + t) * P
-                        nc.tensor.transpose(out=pt[:, t, :], in_=u["xr"][:, i, k0 : k0 + P], identity=ident_f32[:])
-                    u["pt"].append(pt)
+                    for h in range(2):
+                        w0 = (2 * g + h) * P
+                        nc.tensor.transpose(out=pt[:, g, h, :], in_=words[:, w0 : w0 + P], identity=ident_f32[:])
+                u["pt"].append(pt)
 
-        def gather(u, b):
-            size = u["size"]
-            if b == 0:
+        def gather(u, vector):
+            if not vector:
                 u["grouped"] = work.tile([P, UNIT * DIN], BF16, name="grouped", tag="grouped", align_bytes=64)
-            if b < size * PASSES:
-                grouped = u["grouped"][:, 0 : size * DIN].rearrange(
-                    "p (g i m t) -> p g i m t", g=PASSES, i=size, t=PACK
-                )
-                nc.vector.tensor_tensor(
-                    out=grouped[:, b % PASSES, b // PASSES, :, :],
-                    in0=u["pt"][b][:].rearrange("p t m -> p m t"),
-                    in1=gam[:, b % PASSES, :].unsqueeze(1).to_broadcast([P, P, PACK]),
-                    op=ALU.mult,
+            for i in tiles(u):
+                if on_vector(u, i) != vector:
+                    continue
+                copy = nc.vector.tensor_copy if vector else nc.scalar.copy
+                copy(
+                    out=u["grouped"][:, i * DIN : (i + 1) * DIN].bitcast(F32).rearrange(
+                        "p (g m h) -> p g m h", g=PASSES, h=2
+                    ),
+                    in_=u["pt"][i][:].rearrange("p g h m -> p g m h"),
                 )
 
         def quantise(u):
@@ -143,62 +165,22 @@ def tile_bitlinear_t_kernel(tc, x, weight, bias, gamma, out):
             u["codes"], u["scales"] = codes, scales
 
         def multiply(u):
-            size = u["size"]
-            po = ps_o.tile([P, UNIT * DOUT], F32, name="po", tag="po")
-            if u["channels_first"]:
-                for h in range(2):
-                    for g in range(PASSES):
-                        ch = slice(g * DOUT + h * P, g * DOUT + (h + 1) * P)
-                        rows = slice(g * size * P, (g + 1) * size * P)
-                        nc.tensor.matmul_mx(
-                            out=po[:, h * size * P : (h + 1) * size * P],
-                            lhsT=w_codes[:, ch].bitcast(FP8X4), lhsT_scale=w_scales[:, ch],
-                            rhs=u["codes"][:, rows].bitcast(FP8X4), rhs_scale=u["scales"][:, rows],
-                            start=(g == 0), stop=(g == PASSES - 1),
-                        )
-            else:
-                for i in range(size):
-                    for g in range(PASSES):
-                        rows = slice((g * size + i) * P, (g * size + i + 1) * P)
-                        ch = slice(g * DOUT, (g + 1) * DOUT)
-                        nc.tensor.matmul_mx(
-                            out=po[:, i * DOUT : (i + 1) * DOUT],
-                            lhsT=u["codes"][:, rows].bitcast(FP8X4), lhsT_scale=u["scales"][:, rows],
-                            rhs=w_codes[:, ch].bitcast(FP8X4), rhs_scale=w_scales[:, ch],
-                            start=(g == 0), stop=(g == PASSES - 1),
-                        )
-            u["po"] = po
+            u["po"] = ps_o.tile([P, UNIT * DOUT], F32, name="po", tag="po")
+            for i in tiles(u):
+                for g in range(PASSES):
+                    rows = slice((PASSES * i + g) * P, (PASSES * i + g + 1) * P)
+                    ch = slice(g * DOUT, (g + 1) * DOUT)
+                    nc.tensor.matmul_mx(
+                        out=u["po"][:, i * DOUT : (i + 1) * DOUT],
+                        lhsT=u["codes"][:, rows].bitcast(FP8X4), lhsT_scale=u["scales"][:, rows],
+                        rhs=w_codes[:, ch].bitcast(FP8X4), rhs_scale=w_scales[:, ch],
+                        start=(g == 0), stop=(g == PASSES - 1),
+                    )
 
         def add_bias(u):
-            size = u["size"]
-            o_sb = work.tile([P, UNIT * DOUT], F32, name="o_sb", tag="o_sb")
-            if u["channels_first"]:
-                for h in range(2):
-                    cols = slice(h * size * P, (h + 1) * size * P)
-                    nc.scalar.activation(
-                        out=o_sb[:, cols], in_=u["po"][:, cols], func=ACT.Identity, bias=bias_col[:, h : h + 1]
-                    )
-            else:
-                cols = slice(0, size * DOUT)
-                nc.vector.tensor_tensor(out=o_sb[:, cols], in0=u["po"][:, cols], in1=bias2[:, cols], op=ALU.add)
-            u["o_sb"] = o_sb
-
-        def turn_back(u):
-            po = ps_o.tile([P, UNIT * DOUT], F32, name="po", tag="po")
-            for h in range(2):
-                for i in range(u["size"]):
-                    nc.tensor.transpose(
-                        out=po[:, i * DOUT + h * P : i * DOUT + (h + 1) * P],
-                        in_=u["o_sb"][:, (h * u["size"] + i) * P : (h * u["size"] + i + 1) * P],
-                        identity=ident_f32[:],
-                    )
-            u["po"] = po
-
-        def copy_out(u):
+            u["o_sb"] = npool.tile([P, UNIT * DOUT], F32, name="o_sb", tag="o_sb")
             cols = slice(0, u["size"] * DOUT)
-            o_rows = work.tile([P, UNIT * DOUT], F32, name="o_rows", tag="o_rows")
-            nc.scalar.copy(out=o_rows[:, cols], in_=u["po"][:, cols])
-            u["o_sb"] = o_rows
+            nc.vector.tensor_tensor(out=u["o_sb"][:, cols], in0=u["po"][:, cols], in1=bias2[:, cols], op=ALU.add)
 
         def store(u):
             size = u["size"]
@@ -210,24 +192,31 @@ def tile_bitlinear_t_kernel(tc, x, weight, bias, gamma, out):
             )
 
         load(units[0])
+        nc.sync.dma_start(out=vec_rows[0:8, :], in_=gamma.rearrange("(a k) -> a k", k=P))
+        nc.sync.dma_start(out=vec_rows[8:10, :], in_=bias.rearrange("(a k) -> a k", k=P))
         nc.sync.dma_start(out=w_sb[:], in_=weight.rearrange("(h p) k -> p h k", p=P))
         for u in units[1:4]:
             load(u)
 
         vec_ps = ps_t.tile([P, P], BF16, name="vec_ps", tag="pt")
         nc.tensor.transpose(out=vec_ps[:], in_=vec_rows[:], identity=ident[:])
-        gam = const.tile([P, PASSES, PACK], F32)
-        nc.vector.tensor_copy(out=gam[:].rearrange("p g t -> p (g t)"), in_=vec_ps[:, 0:8])
-        bias_col = const.tile([P, 2], F32)
-        nc.vector.tensor_copy(out=bias_col[:], in_=vec_ps[:, 8:10])
-        bias_t = const.tile([P, 2, P], F32)
-        nc.vector.tensor_copy(out=bias_t[:], in_=vec_ps[:, 8:10].unsqueeze(2).to_broadcast([P, 2, P]))
-        bias_ps = ps_o.tile([P, UNIT, DOUT], F32, name="bias_ps", tag="po")
+        vec_cols = const.tile([P, 10], BF16)
+        nc.vector.tensor_copy(out=vec_cols[:], in_=vec_ps[:, 0:10])
+        gam_ps = ps_g.tile([P, DIN], BF16)
+        for a in range(8):
+            nc.tensor.transpose(
+                out=gam_ps[:, a * P : (a + 1) * P], in_=vec_cols[:, a : a + 1].to_broadcast([P, P]), identity=ident[:]
+            )
+        gam_rows = const.tile([P, DIN], BF16)
+        bias_ps = ps_t.tile([P, DOUT], BF16, name="bias_ps", tag="pt")
+        for h in range(2):
+            nc.tensor.transpose(
+                out=bias_ps[:, h * P : (h + 1) * P], in_=vec_cols[:, 8 + h : 9 + h].to_broadcast([P, P]),
+                identity=ident[:],
+            )
+        bias2 = const.tile([P, UNIT * DOUT], F32)
         for i in range(UNIT):
-            for h in range(2):
-                nc.tensor.transpose(
-                    out=bias_ps[:, i, h * P : (h + 1) * P], in_=bias_t[:, h, :], identity=ident_f32[:]
-                )
+            nc.vector.tensor_copy(out=bias2[:, i * DOUT : (i + 1) * DOUT], in_=bias_ps[:])
 
         abs_sum = const.tile([P, 2], F32)
         for h in range(2):
@@ -260,7 +249,8 @@ def tile_bitlinear_t_kernel(tc, x, weight, bias, gamma, out):
                 for g in range(PASSES):
                     w_ps = ps_t.tile([P, PACK, P], F32, name="w_ps", tag="pt")
                     for t in range(PACK):
-                        k_cols = slice((g * PACK + t) * P, (g * PACK + t + 1) * P)
+                        k0 = g * P * PACK + (t // 2) * 2 * P + t % 2
+                        k_cols = slice(k0, k0 + 2 * P - 1, 2)
                         nc.tensor.matmul(w_ps[:, t, :], lhsT=w_pos[:, h, k_cols], rhs=ident[:], start=True, stop=False)
                         nc.tensor.matmul(w_ps[:, t, :], lhsT=w_neg[:, h, k_cols], rhs=neg_ident[:], start=False, stop=True)
                     nc.scalar.copy(
@@ -273,48 +263,42 @@ def tile_bitlinear_t_kernel(tc, x, weight, bias, gamma, out):
                 in_=w_grouped[:].rearrange("p g n t -> p (g n t)"),
             )
 
-        bias2 = const.tile([P, UNIT * DOUT], F32)
-        nc.vector.tensor_copy(out=bias2[:], in_=bias_ps[:].rearrange("p i c -> p (i c)"))
-
         def at(i):
             return units[i] if 0 <= i < len(units) else None
 
-        for s in range(len(units) + 8):
-            new, scale, now, quant, mult, bias_u, back, last = [at(s - d) for d in range(8)]
+        for s in range(len(units) + 7):
+            new, norm, turned, gathered, quant, mult, done = [at(s - d) for d in (0, 1, 3, 4, 5, 6, 7)]
+            if s == 1:
+                nc.scalar.copy(out=gam_rows[:], in_=gam_ps[:])
+            if norm:
+                times_rstd(norm)
             if new:
+                times_gamma(new)
                 square(new, 0)
-            if bias_u and bias_u["channels_first"]:
-                add_bias(bias_u)
+            if gathered:
+                gather(gathered, False)
             if new:
                 square(new, 1)
                 root(new)
-            if last and last["channels_first"]:
-                copy_out(last)
-            if scale:
-                scale_rows(scale)
-            if now:
-                turn(now)
-                gather(now, 0)
+            if norm:
+                normalise(norm, 0)
             if quant:
                 quantise(quant)
-            if s == 4:
+            if s == 5:
                 quantise_weights()
-            if now:
-                gather(now, 1)
-                gather(now, 2)
-            if bias_u and not bias_u["channels_first"]:
-                add_bias(bias_u)
-            if now:
-                gather(now, 3)
-            if back and back["channels_first"]:
-                turn_back(back)
+            if norm:
+                normalise(norm, 1)
+            if done:
+                add_bias(done)
+            if gathered:
+                gather(gathered, True)
+            if turned:
+                turn(turned)
             if s == 3:
                 turn_weights()
             if mult:
                 multiply(mult)
-            if bias_u and not bias_u["channels_first"]:
-                store(bias_u)
-            if last and last["channels_first"]:
-                store(last)
+            if done:
+                store(done)
             if s >= 1 and at(s + 3):
                 load(at(s + 3))

@@ -23,8 +23,6 @@ PASSES = 2
 PACK = 4
 CHUNKS = [1, 1, 2] + [4] * 14 + [2, 1, 1]
 UNIT = 2
-GPSIMD_EVERY = 3
-VECTOR_COPY_EVERY = 4
 
 
 def tile_bitlinear_t_kernel(tc, x, weight, bias, gamma, out):
@@ -41,7 +39,7 @@ def tile_bitlinear_t_kernel(tc, x, weight, bias, gamma, out):
         small = ctx.enter_context(tc.tile_pool(name="small", bufs=4))
         ps_t = ctx.enter_context(tc.psum_pool(name="ps_t", bufs=4))
         ps_g = ctx.enter_context(tc.psum_pool(name="ps_g", bufs=1))
-        ps_o = ctx.enter_context(tc.psum_pool(name="ps_o", bufs=3))
+        ps_o = ctx.enter_context(tc.psum_pool(name="ps_o", bufs=2))
 
         ctx.enter_context(tc.manual_schedule())
 
@@ -99,31 +97,10 @@ def tile_bitlinear_t_kernel(tc, x, weight, bias, gamma, out):
         def tiles(u):
             return range(u["size"])
 
-        def on_gpsimd(u, i):
-            return (u["base"] + u["r"] + i) % GPSIMD_EVERY == GPSIMD_EVERY - 1
-
-        def on_vector(u, i):
-            return (u["base"] + u["r"] + i) % VECTOR_COPY_EVERY == VECTOR_COPY_EVERY - 1
-
-        def times_gamma(u):
-            u["xn"] = npool.tile([P, UNIT, DIN], BF16, name="xn", tag="xn")
-            for i in tiles(u):
-                if on_gpsimd(u, i):
-                    u["xg"] = work.tile([P, DIN], F32, name="xg", tag="xg")
-                    nc.gpsimd.tensor_tensor(
-                        out=u["xg"][:], in0=chunk_of[u["base"]][:, u["r"] + i, :], in1=gam_rows[:], op=ALU.mult
-                    )
-
-        def times_rstd(u):
-            for i in tiles(u):
-                if on_gpsimd(u, i):
-                    nc.gpsimd.tensor_scalar(
-                        out=u["xn"][:, i, :], in0=u["xg"][:], scalar1=u["rstd"][:, i : i + 1], scalar2=1.0,
-                        op0=ALU.mult, op1=ALU.mult,
-                    )
-
         def normalise(u, i):
-            if i < u["size"] and not on_gpsimd(u, i):
+            if i == 0:
+                u["xn"] = npool.tile([P, UNIT, DIN], BF16, name="xn", tag="xn")
+            if i < u["size"]:
                 nc.vector.scalar_tensor_tensor(
                     out=u["xn"][:, i, :], in0=chunk_of[u["base"]][:, u["r"] + i, :],
                     scalar=u["rstd"][:, i : i + 1], in1=gam_ps[:], op0=ALU.mult, op1=ALU.mult,
@@ -140,14 +117,11 @@ def tile_bitlinear_t_kernel(tc, x, weight, bias, gamma, out):
                         nc.tensor.transpose(out=pt[:, g, h, :], in_=words[:, w0 : w0 + P], identity=ident_f32[:])
                 u["pt"].append(pt)
 
-        def gather(u, vector):
-            if not vector:
+        def gather(u, i):
+            if i == 0:
                 u["grouped"] = work.tile([P, UNIT * DIN], BF16, name="grouped", tag="grouped", align_bytes=64)
-            for i in tiles(u):
-                if on_vector(u, i) != vector:
-                    continue
-                copy = nc.vector.tensor_copy if vector else nc.scalar.copy
-                copy(
+            if i < u["size"]:
+                nc.scalar.copy(
                     out=u["grouped"][:, i * DIN : (i + 1) * DIN].bitcast(F32).rearrange(
                         "p (g m h) -> p g m h", g=PASSES, h=2
                     ),
@@ -207,16 +181,13 @@ def tile_bitlinear_t_kernel(tc, x, weight, bias, gamma, out):
             nc.tensor.transpose(
                 out=gam_ps[:, a * P : (a + 1) * P], in_=vec_cols[:, a : a + 1].to_broadcast([P, P]), identity=ident[:]
             )
-        gam_rows = const.tile([P, DIN], BF16)
-        bias_ps = ps_t.tile([P, DOUT], BF16, name="bias_ps", tag="pt")
+        bias_ps = ps_g.tile([P, DOUT], BF16, name="bias_ps", tag="bias_ps")
         for h in range(2):
             nc.tensor.transpose(
                 out=bias_ps[:, h * P : (h + 1) * P], in_=vec_cols[:, 8 + h : 9 + h].to_broadcast([P, P]),
                 identity=ident[:],
             )
         bias2 = const.tile([P, UNIT * DOUT], F32)
-        for i in range(UNIT):
-            nc.vector.tensor_copy(out=bias2[:, i * DOUT : (i + 1) * DOUT], in_=bias_ps[:])
 
         abs_sum = const.tile([P, 2], F32)
         for h in range(2):
@@ -233,29 +204,33 @@ def tile_bitlinear_t_kernel(tc, x, weight, bias, gamma, out):
         nc.vector.tensor_scalar(out=nthr[:], in0=total[:], scalar1=-1.0 / (DOUT * DIN), scalar2=None, op0=ALU.mult)
         w_flat = w_sb[:].rearrange("p h k -> p (h k)")
         w_pos = const.tile([P, 2, DIN], BF16)
-        nc.vector.tensor_scalar(
-            out=w_pos[:].rearrange("p h k -> p (h k)"), in0=w_flat, scalar1=thr[:, 0:1], scalar2=None, op0=ALU.is_gt
-        )
         w_neg = const.tile([P, 2, DIN], BF16)
-        nc.vector.tensor_scalar(
-            out=w_neg[:].rearrange("p h k -> p (h k)"), in0=w_flat, scalar1=nthr[:, 0:1], scalar2=None, op0=ALU.is_lt
-        )
+
+        def ternary_masks():
+            for mask, limit, op in ((w_pos, thr, ALU.is_gt), (w_neg, nthr, ALU.is_lt)):
+                nc.vector.tensor_scalar(
+                    out=mask[:].rearrange("p h k -> p (h k)"), in0=w_flat, scalar1=limit[:, 0:1], scalar2=None, op0=op
+                )
+
         w_grouped = const.tile([P, PASSES, DOUT, PACK], BF16, align_bytes=64)
         w_codes = const.tile([P, PASSES * DOUT], U32, align_bytes=64)
         w_scales = const.tile([P, PASSES * DOUT], U8, align_bytes=64)
 
-        def turn_weights():
-            for h in range(2):
-                for g in range(PASSES):
-                    w_ps = ps_t.tile([P, PACK, P], F32, name="w_ps", tag="pt")
-                    for t in range(PACK):
-                        k0 = g * P * PACK + (t // 2) * 2 * P + t % 2
-                        k_cols = slice(k0, k0 + 2 * P - 1, 2)
-                        nc.tensor.matmul(w_ps[:, t, :], lhsT=w_pos[:, h, k_cols], rhs=ident[:], start=True, stop=False)
-                        nc.tensor.matmul(w_ps[:, t, :], lhsT=w_neg[:, h, k_cols], rhs=neg_ident[:], start=False, stop=True)
-                    nc.scalar.copy(
-                        out=w_grouped[:, g, h * P : (h + 1) * P, :], in_=w_ps[:].rearrange("p t n -> p n t")
-                    )
+        w_turned = {}
+
+        def turn_weights(g, h):
+            w_ps = ps_o.tile([P, PACK, P], F32, name="w_ps", tag="po")
+            for t in range(PACK):
+                k0 = g * P * PACK + (t // 2) * 2 * P + t % 2
+                k_cols = slice(k0, k0 + 2 * P - 1, 2)
+                nc.tensor.matmul(w_ps[:, t, :], lhsT=w_pos[:, h, k_cols], rhs=ident[:], start=True, stop=False)
+                nc.tensor.matmul(w_ps[:, t, :], lhsT=w_neg[:, h, k_cols], rhs=neg_ident[:], start=False, stop=True)
+            w_turned[g, h] = w_ps
+
+        def gather_weights(g, h):
+            nc.scalar.copy(
+                out=w_grouped[:, g, h * P : (h + 1) * P, :], in_=w_turned[g, h][:].rearrange("p t n -> p n t")
+            )
 
         def quantise_weights():
             nc.vector.quantize_mx(
@@ -268,34 +243,38 @@ def tile_bitlinear_t_kernel(tc, x, weight, bias, gamma, out):
 
         for s in range(len(units) + 7):
             new, norm, turned, gathered, quant, mult, done = [at(s - d) for d in (0, 1, 3, 4, 5, 6, 7)]
-            if s == 1:
-                nc.scalar.copy(out=gam_rows[:], in_=gam_ps[:])
-            if norm:
-                times_rstd(norm)
             if new:
-                times_gamma(new)
                 square(new, 0)
             if gathered:
-                gather(gathered, False)
+                gather(gathered, 0)
             if new:
                 square(new, 1)
                 root(new)
+            if gathered:
+                gather(gathered, 1)
+            if s in (4, 5):
+                gather_weights(s - 4, 0)
+                gather_weights(s - 4, 1)
             if norm:
                 normalise(norm, 0)
+            if s == 1:
+                ternary_masks()
             if quant:
                 quantise(quant)
-            if s == 5:
+            if s == 6:
                 quantise_weights()
             if norm:
                 normalise(norm, 1)
+            if s == 5:
+                for i in range(UNIT):
+                    nc.vector.tensor_copy(out=bias2[:, i * DOUT : (i + 1) * DOUT], in_=bias_ps[:])
             if done:
                 add_bias(done)
-            if gathered:
-                gather(gathered, True)
             if turned:
                 turn(turned)
-            if s == 3:
-                turn_weights()
+            if s in (3, 4):
+                turn_weights(s - 3, 0)
+                turn_weights(s - 3, 1)
             if mult:
                 multiply(mult)
             if done:

@@ -23,6 +23,8 @@ PASSES = 2
 PACK = 4
 CHUNKS = [1, 1, 2] + [4] * 14 + [2, 1, 1]
 UNIT = 2
+GPSIMD_EVERY = 4
+VECTOR_COPY_EVERY = 4
 
 
 def tile_bitlinear_t_kernel(tc, x, weight, bias, gamma, out):
@@ -61,10 +63,9 @@ def tile_bitlinear_t_kernel(tc, x, weight, bias, gamma, out):
         units = []
         row_tile = 0
         for n in CHUNKS:
+            chunk = {}
             for r in range(0, n, UNIT):
-                units.append({
-                    "base": row_tile, "n": n, "r": r, "size": min(UNIT, n - r),
-                })
+                units.append({"base": row_tile, "n": n, "r": r, "size": min(UNIT, n - r), "chunk": chunk})
             row_tile += n
         chunk_of = {}
 
@@ -97,10 +98,31 @@ def tile_bitlinear_t_kernel(tc, x, weight, bias, gamma, out):
         def tiles(u):
             return range(u["size"])
 
+        def on_gpsimd(u, i):
+            return (u["base"] + u["r"] + i) % GPSIMD_EVERY == 2
+
+        def on_vector(u, i):
+            return (u["base"] + u["r"] + i) % VECTOR_COPY_EVERY == 0
+
+        def times_gamma(u):
+            u["xn"] = npool.tile([P, UNIT, DIN], BF16, name="xn", tag="xn")
+            for i in tiles(u):
+                if on_gpsimd(u, i):
+                    u["xg"] = work.tile([P, DIN], F32, name="xg", tag="xg")
+                    nc.gpsimd.tensor_tensor(
+                        out=u["xg"][:], in0=chunk_of[u["base"]][:, u["r"] + i, :], in1=gam_rows[:], op=ALU.mult
+                    )
+
+        def times_rstd(u):
+            for i in tiles(u):
+                if on_gpsimd(u, i):
+                    nc.gpsimd.tensor_scalar(
+                        out=u["xn"][:, i, :], in0=u["xg"][:], scalar1=u["rstd"][:, i : i + 1], scalar2=1.0,
+                        op0=ALU.mult, op1=ALU.mult,
+                    )
+
         def normalise(u, i):
-            if i == 0:
-                u["xn"] = npool.tile([P, UNIT, DIN], BF16, name="xn", tag="xn")
-            if i < u["size"]:
+            if i < u["size"] and not on_gpsimd(u, i):
                 nc.vector.scalar_tensor_tensor(
                     out=u["xn"][:, i, :], in0=chunk_of[u["base"]][:, u["r"] + i, :],
                     scalar=u["rstd"][:, i : i + 1], in1=gam_ps[:], op0=ALU.mult, op1=ALU.mult,
@@ -118,35 +140,40 @@ def tile_bitlinear_t_kernel(tc, x, weight, bias, gamma, out):
                 u["pt"].append(pt)
 
         def gather(u, i):
-            if i == 0:
-                u["grouped"] = work.tile([P, UNIT * DIN], BF16, name="grouped", tag="grouped", align_bytes=64)
+            if i == 0 and u["r"] == 0:
+                u["chunk"]["grouped"] = work.tile([P, 4 * DIN], BF16, name="grouped", tag="grouped", align_bytes=64)
             if i < u["size"]:
-                nc.scalar.copy(
-                    out=u["grouped"][:, i * DIN : (i + 1) * DIN].bitcast(F32).rearrange(
+                r = u["r"] + i
+                copy = nc.vector.tensor_copy if on_vector(u, i) else nc.scalar.copy
+                copy(
+                    out=u["chunk"]["grouped"][:, r * DIN : (r + 1) * DIN].bitcast(F32).rearrange(
                         "p (g m h) -> p g m h", g=PASSES, h=2
                     ),
                     in_=u["pt"][i][:].rearrange("p g h m -> p g m h"),
                 )
 
         def quantise(u):
-            codes = work.tile([P, UNIT * PASSES * P], U32, name="codes", tag="codes", align_bytes=64)
-            scales = work.tile([P, UNIT * PASSES * P], U8, name="scales", tag="scales", align_bytes=64)
-            width = u["size"] * PASSES * P
+            if u["r"] + u["size"] < u["n"]:
+                return
+            codes = work.tile([P, 4 * PASSES * P], U32, name="codes", tag="codes", align_bytes=64)
+            scales = work.tile([P, 4 * PASSES * P], U8, name="scales", tag="scales", align_bytes=64)
+            width = u["n"] * PASSES * P
             nc.vector.quantize_mx(
                 out=codes[:, 0:width].bitcast(FP8X4), scales=scales[:, 0:width],
-                in_=u["grouped"][:, 0 : width * PACK],
+                in_=u["chunk"]["grouped"][:, 0 : width * PACK],
             )
-            u["codes"], u["scales"] = codes, scales
+            u["chunk"]["codes"], u["chunk"]["scales"] = codes, scales
 
         def multiply(u):
             u["po"] = ps_o.tile([P, UNIT * DOUT], F32, name="po", tag="po")
             for i in tiles(u):
                 for g in range(PASSES):
-                    rows = slice((PASSES * i + g) * P, (PASSES * i + g + 1) * P)
+                    word0 = (PASSES * (u["r"] + i) + g) * P
+                    rows = slice(word0, word0 + P)
                     ch = slice(g * DOUT, (g + 1) * DOUT)
                     nc.tensor.matmul_mx(
                         out=u["po"][:, i * DOUT : (i + 1) * DOUT],
-                        lhsT=u["codes"][:, rows].bitcast(FP8X4), lhsT_scale=u["scales"][:, rows],
+                        lhsT=u["chunk"]["codes"][:, rows].bitcast(FP8X4), lhsT_scale=u["chunk"]["scales"][:, rows],
                         rhs=w_codes[:, ch].bitcast(FP8X4), rhs_scale=w_scales[:, ch],
                         start=(g == 0), stop=(g == PASSES - 1),
                     )
@@ -181,6 +208,7 @@ def tile_bitlinear_t_kernel(tc, x, weight, bias, gamma, out):
             nc.tensor.transpose(
                 out=gam_ps[:, a * P : (a + 1) * P], in_=vec_cols[:, a : a + 1].to_broadcast([P, P]), identity=ident[:]
             )
+        gam_rows = const.tile([P, DIN], BF16)
         bias_ps = ps_g.tile([P, DOUT], BF16, name="bias_ps", tag="bias_ps")
         for h in range(2):
             nc.tensor.transpose(
@@ -189,19 +217,28 @@ def tile_bitlinear_t_kernel(tc, x, weight, bias, gamma, out):
             )
         bias2 = const.tile([P, UNIT * DOUT], F32)
 
-        abs_sum = const.tile([P, 2], F32)
-        for h in range(2):
-            nc.vector.tensor_reduce(
-                out=abs_sum[:, h : h + 1], in_=w_sb[:, h, :], axis=AX.X, op=ALU.add, apply_absolute_value=True
+        half_sign = const.tile([P, 2 * DIN], BF16)
+        nc.vector.tensor_scalar(
+            out=half_sign[:], in0=w_sb[:].rearrange("p h k -> p (h k)"), scalar1=0.0, scalar2=0.5,
+            op0=ALU.is_ge, op1=ALU.subtract,
+        )
+        gram = ps_o.tile([P, P], F32, name="gram", tag="po")
+        for b in range(2 * DIN // P):
+            nc.tensor.matmul(
+                gram[:], lhsT=w_sb[:].rearrange("p h k -> p (h k)")[:, b * P : (b + 1) * P],
+                rhs=half_sign[:, b * P : (b + 1) * P], start=(b == 0), stop=(b == 2 * DIN // P - 1),
             )
-        tot = ps_o.tile([P, 2], F32, name="tot", tag="po")
-        nc.tensor.matmul(tot[:], lhsT=ones[:], rhs=abs_sum[:], start=True, stop=True)
-        total = const.tile([P, 1], F32)
-        nc.vector.tensor_reduce(out=total[:], in_=tot[:], axis=AX.X, op=ALU.add)
+        diag = const.tile([P, P], F32)
+        diag_sum = const.tile([P, 1], F32)
+        nc.vector.scalar_tensor_tensor(
+            out=diag[:], in0=gram[:], scalar=1.0, in1=ident_f32[:], op0=ALU.mult, op1=ALU.mult, accum_out=diag_sum[:]
+        )
+        tot = ps_o.tile([P, 1], F32, name="tot", tag="po")
+        nc.tensor.matmul(tot[:], lhsT=ones[:], rhs=diag_sum[:], start=True, stop=True)
         thr = const.tile([P, 1], F32)
-        nc.vector.tensor_scalar(out=thr[:], in0=total[:], scalar1=1.0 / (DOUT * DIN), scalar2=None, op0=ALU.mult)
+        nc.vector.tensor_scalar(out=thr[:], in0=tot[:], scalar1=2.0 / (DOUT * DIN), scalar2=None, op0=ALU.mult)
         nthr = const.tile([P, 1], F32)
-        nc.vector.tensor_scalar(out=nthr[:], in0=total[:], scalar1=-1.0 / (DOUT * DIN), scalar2=None, op0=ALU.mult)
+        nc.vector.tensor_scalar(out=nthr[:], in0=tot[:], scalar1=-2.0 / (DOUT * DIN), scalar2=None, op0=ALU.mult)
         w_flat = w_sb[:].rearrange("p h k -> p (h k)")
         w_pos = const.tile([P, 2, DIN], BF16)
         w_neg = const.tile([P, 2, DIN], BF16)
@@ -241,17 +278,20 @@ def tile_bitlinear_t_kernel(tc, x, weight, bias, gamma, out):
         def at(i):
             return units[i] if 0 <= i < len(units) else None
 
-        for s in range(len(units) + 7):
-            new, norm, turned, gathered, quant, mult, done = [at(s - d) for d in (0, 1, 3, 4, 5, 6, 7)]
+        for s in range(len(units) + 8):
+            new, norm, turned, gathered, quant, mult, done = [at(s - d) for d in (0, 1, 3, 4, 5, 7, 8)]
+            if s == 1:
+                nc.scalar.copy(out=gam_rows[:], in_=gam_ps[:])
+            if norm:
+                times_rstd(norm)
             if new:
+                times_gamma(new)
                 square(new, 0)
-            if gathered:
+            if gathered and not on_vector(gathered, 0):
                 gather(gathered, 0)
             if new:
                 square(new, 1)
                 root(new)
-            if gathered:
-                gather(gathered, 1)
             if s in (4, 5):
                 gather_weights(s - 4, 0)
                 gather_weights(s - 4, 1)
@@ -268,6 +308,10 @@ def tile_bitlinear_t_kernel(tc, x, weight, bias, gamma, out):
             if s == 5:
                 for i in range(UNIT):
                     nc.vector.tensor_copy(out=bias2[:, i * DOUT : (i + 1) * DOUT], in_=bias_ps[:])
+            if gathered and on_vector(gathered, 0):
+                gather(gathered, 0)
+            if gathered:
+                gather(gathered, 1)
             if done:
                 add_bias(done)
             if turned:

@@ -23,8 +23,6 @@ PASSES = 2
 PACK = 4
 CHUNKS = [1, 1, 2] + [4] * 14 + [2, 1, 1]
 UNIT = 2
-GPSIMD_EVERY = 4
-VECTOR_COPY_EVERY = 4
 
 
 def tile_bitlinear_t_kernel(tc, x, weight, bias, gamma, out):
@@ -99,13 +97,25 @@ def tile_bitlinear_t_kernel(tc, x, weight, bias, gamma, out):
             return range(u["size"])
 
         def on_gpsimd(u, i):
-            return (u["base"] + u["r"] + i) % GPSIMD_EVERY == 2
+            return u["n"] == 4 and u["r"] + i == 0
 
         def on_vector(u, i):
-            return (u["base"] + u["r"] + i) % VECTOR_COPY_EVERY == 0
+            return late_gamma(u, i) or u["base"] < 32 and u["base"] % 8 == 4 and u["r"] + i == 1
+
+        def late_gamma(u, i):
+            return u["n"] == 4 and u["r"] + i == 2
+
+        def times_rstd_only(u):
+            for i in tiles(u):
+                if late_gamma(u, i):
+                    u["xr"] = work.tile([P, DIN], F32, name="xr", tag="grouped", align_bytes=64)
+                    nc.gpsimd.tensor_scalar(
+                        out=u["xr"][:].rearrange("p (a e q) -> p a e q", a=4, e=2),
+                        in0=chunk_of[u["base"]][:, u["r"] + i, :].rearrange("p (a q e) -> p a e q", a=4, e=2),
+                        scalar1=u["rstd"][:, i : i + 1], scalar2=1.0, op0=ALU.mult, op1=ALU.mult,
+                    )
 
         def times_gamma(u):
-            u["xn"] = npool.tile([P, UNIT, DIN], BF16, name="xn", tag="xn")
             for i in tiles(u):
                 if on_gpsimd(u, i):
                     u["xg"] = work.tile([P, DIN], F32, name="xg", tag="xg")
@@ -122,7 +132,7 @@ def tile_bitlinear_t_kernel(tc, x, weight, bias, gamma, out):
                     )
 
         def normalise(u, i):
-            if i < u["size"] and not on_gpsimd(u, i):
+            if i < u["size"] and not on_gpsimd(u, i) and not late_gamma(u, i):
                 nc.vector.scalar_tensor_tensor(
                     out=u["xn"][:, i, :], in0=chunk_of[u["base"]][:, u["r"] + i, :],
                     scalar=u["rstd"][:, i : i + 1], in1=gam_ps[:], op0=ALU.mult, op1=ALU.mult,
@@ -131,6 +141,16 @@ def tile_bitlinear_t_kernel(tc, x, weight, bias, gamma, out):
         def turn(u):
             u["pt"] = []
             for i in tiles(u):
+                if late_gamma(u, i):
+                    pair = []
+                    for g in range(PASSES):
+                        pt = ps_t.tile([P, PACK, P], F32, name="pt", tag="pt")
+                        for t in range(PACK):
+                            c0 = (PACK * g + t) * P
+                            nc.tensor.transpose(out=pt[:, t, :], in_=u["xr"][:, c0 : c0 + P], identity=ident_f32[:])
+                        pair.append(pt)
+                    u["pt"].append(pair)
+                    continue
                 words = u["xn"][:, i, :].bitcast(F32)
                 pt = ps_t.tile([P, PASSES, 2, P], F32, name="pt", tag="pt")
                 for g in range(PASSES):
@@ -139,12 +159,19 @@ def tile_bitlinear_t_kernel(tc, x, weight, bias, gamma, out):
                         nc.tensor.transpose(out=pt[:, g, h, :], in_=words[:, w0 : w0 + P], identity=ident_f32[:])
                 u["pt"].append(pt)
 
-        def gather(u, i):
-            if i == 0 and u["r"] == 0:
-                u["chunk"]["grouped"] = work.tile([P, 4 * DIN], BF16, name="grouped", tag="grouped", align_bytes=64)
-            if i < u["size"]:
+        def gather(u, i, vector):
+            if u and i < u["size"] and on_vector(u, i) == vector:
                 r = u["r"] + i
-                copy = nc.vector.tensor_copy if on_vector(u, i) else nc.scalar.copy
+                if late_gamma(u, i):
+                    for g in range(PASSES):
+                        c0 = r * DIN + g * P * PACK
+                        nc.vector.tensor_tensor(
+                            out=u["chunk"]["grouped"][:, c0 : c0 + P * PACK].rearrange("p (m t) -> p m t", t=PACK),
+                            in0=u["pt"][i][g][:].rearrange("p t m -> p m t"),
+                            in1=gam_k[:, g, :].unsqueeze(1).to_broadcast([P, P, PACK]), op=ALU.mult,
+                        )
+                    return
+                copy = nc.vector.tensor_copy if vector else nc.scalar.copy
                 copy(
                     out=u["chunk"]["grouped"][:, r * DIN : (r + 1) * DIN].bitcast(F32).rearrange(
                         "p (g m h) -> p g m h", g=PASSES, h=2
@@ -195,9 +222,10 @@ def tile_bitlinear_t_kernel(tc, x, weight, bias, gamma, out):
         load(units[0])
         nc.sync.dma_start(out=vec_rows[0:8, :], in_=gamma.rearrange("(a k) -> a k", k=P))
         nc.sync.dma_start(out=vec_rows[8:10, :], in_=bias.rearrange("(a k) -> a k", k=P))
-        nc.sync.dma_start(out=w_sb[:], in_=weight.rearrange("(h p) k -> p h k", p=P))
-        for u in units[1:4]:
+        for u in units[1:3]:
             load(u)
+        nc.sync.dma_start(out=w_sb[:], in_=weight.rearrange("(h p) k -> p h k", p=P))
+        load(units[3])
 
         vec_ps = ps_t.tile([P, P], BF16, name="vec_ps", tag="pt")
         nc.tensor.transpose(out=vec_ps[:], in_=vec_rows[:], identity=ident[:])
@@ -215,30 +243,39 @@ def tile_bitlinear_t_kernel(tc, x, weight, bias, gamma, out):
                 out=bias_ps[:, h * P : (h + 1) * P], in_=vec_cols[:, 8 + h : 9 + h].to_broadcast([P, P]),
                 identity=ident[:],
             )
+        gam_k = const.tile([P, PASSES, PACK], F32)
         bias2 = const.tile([P, UNIT * DOUT], F32)
 
         half_sign = const.tile([P, 2 * DIN], BF16)
-        nc.vector.tensor_scalar(
-            out=half_sign[:], in0=w_sb[:].rearrange("p h k -> p (h k)"), scalar1=0.0, scalar2=0.5,
-            op0=ALU.is_ge, op1=ALU.subtract,
-        )
         gram = ps_o.tile([P, P], F32, name="gram", tag="po")
-        for b in range(2 * DIN // P):
-            nc.tensor.matmul(
-                gram[:], lhsT=w_sb[:].rearrange("p h k -> p (h k)")[:, b * P : (b + 1) * P],
-                rhs=half_sign[:, b * P : (b + 1) * P], start=(b == 0), stop=(b == 2 * DIN // P - 1),
+
+        def trace():
+            nc.vector.tensor_scalar(
+                out=half_sign[:], in0=w_sb[:].rearrange("p h k -> p (h k)"), scalar1=0.0, scalar2=0.5,
+                op0=ALU.is_ge, op1=ALU.subtract,
             )
-        diag = const.tile([P, P], F32)
-        diag_sum = const.tile([P, 1], F32)
-        nc.vector.scalar_tensor_tensor(
-            out=diag[:], in0=gram[:], scalar=1.0, in1=ident_f32[:], op0=ALU.mult, op1=ALU.mult, accum_out=diag_sum[:]
-        )
-        tot = ps_o.tile([P, 1], F32, name="tot", tag="po")
-        nc.tensor.matmul(tot[:], lhsT=ones[:], rhs=diag_sum[:], start=True, stop=True)
+            for b in range(2 * DIN // P):
+                nc.tensor.matmul(
+                    gram[:], lhsT=w_sb[:].rearrange("p h k -> p (h k)")[:, b * P : (b + 1) * P],
+                    rhs=half_sign[:, b * P : (b + 1) * P], start=(b == 0), stop=(b == 2 * DIN // P - 1),
+                )
+
         thr = const.tile([P, 1], F32)
-        nc.vector.tensor_scalar(out=thr[:], in0=tot[:], scalar1=2.0 / (DOUT * DIN), scalar2=None, op0=ALU.mult)
         nthr = const.tile([P, 1], F32)
-        nc.vector.tensor_scalar(out=nthr[:], in0=tot[:], scalar1=-2.0 / (DOUT * DIN), scalar2=None, op0=ALU.mult)
+
+        def threshold():
+            diag = const.tile([P, P], F32)
+            diag_sum = const.tile([P, 1], F32)
+            nc.vector.scalar_tensor_tensor(
+                out=diag[:], in0=gram[:], scalar=1.0, in1=ident_f32[:], op0=ALU.mult, op1=ALU.mult,
+                accum_out=diag_sum[:],
+            )
+            tot = ps_o.tile([P, 1], F32, name="tot", tag="po")
+            nc.tensor.matmul(tot[:], lhsT=ones[:], rhs=diag_sum[:], start=True, stop=True)
+            mean = 2.0 / (DOUT * DIN)
+            nc.vector.tensor_scalar(out=thr[:], in0=tot[:], scalar1=mean, scalar2=None, op0=ALU.mult)
+            nc.vector.tensor_scalar(out=nthr[:], in0=tot[:], scalar1=-mean, scalar2=None, op0=ALU.mult)
+
         w_flat = w_sb[:].rearrange("p h k -> p (h k)")
         w_pos = const.tile([P, 2, DIN], BF16)
         w_neg = const.tile([P, 2, DIN], BF16)
@@ -253,21 +290,31 @@ def tile_bitlinear_t_kernel(tc, x, weight, bias, gamma, out):
         w_codes = const.tile([P, PASSES * DOUT], U32, align_bytes=64)
         w_scales = const.tile([P, PASSES * DOUT], U8, align_bytes=64)
 
+        gam_turned = []
         w_turned = {}
 
-        def turn_weights(g, h):
-            w_ps = ps_o.tile([P, PACK, P], F32, name="w_ps", tag="po")
-            for t in range(PACK):
-                k0 = g * P * PACK + (t // 2) * 2 * P + t % 2
-                k_cols = slice(k0, k0 + 2 * P - 1, 2)
-                nc.tensor.matmul(w_ps[:, t, :], lhsT=w_pos[:, h, k_cols], rhs=ident[:], start=True, stop=False)
-                nc.tensor.matmul(w_ps[:, t, :], lhsT=w_neg[:, h, k_cols], rhs=neg_ident[:], start=False, stop=True)
-            w_turned[g, h] = w_ps
+        def turn_gamma():
+            gt = ps_o.tile([P, 2 * PACK, P], BF16, name="gt", tag="po")
+            for j in range(2 * PACK):
+                k0 = j // 2 * 2 * P + j % 2
+                nc.tensor.transpose(out=gt[:, j, :], in_=gam_rows[:, k0 : k0 + 2 * P - 1 : 2], identity=ident[:])
+            gam_turned.append(gt)
 
-        def gather_weights(g, h):
-            nc.scalar.copy(
-                out=w_grouped[:, g, h * P : (h + 1) * P, :], in_=w_turned[g, h][:].rearrange("p t n -> p n t")
-            )
+        def turn_weights(g):
+            for h in range(2):
+                w_ps = ps_t.tile([P, PACK, P], F32, name="w_ps", tag="pt")
+                for t in range(PACK):
+                    k0 = g * P * PACK + (t // 2) * 2 * P + t % 2
+                    k_cols = slice(k0, k0 + 2 * P - 1, 2)
+                    nc.tensor.matmul(w_ps[:, t, :], lhsT=w_pos[:, h, k_cols], rhs=ident[:], start=True, stop=False)
+                    nc.tensor.matmul(w_ps[:, t, :], lhsT=w_neg[:, h, k_cols], rhs=neg_ident[:], start=False, stop=True)
+                w_turned[g, h] = w_ps
+
+        def gather_weights(g):
+            for h in range(2):
+                nc.vector.tensor_copy(
+                    out=w_grouped[:, g, h * P : (h + 1) * P, :], in_=w_turned[g, h][:].rearrange("p t n -> p n t")
+                )
 
         def quantise_weights():
             nc.vector.quantize_mx(
@@ -278,47 +325,56 @@ def tile_bitlinear_t_kernel(tc, x, weight, bias, gamma, out):
         def at(i):
             return units[i] if 0 <= i < len(units) else None
 
-        for s in range(len(units) + 8):
-            new, norm, turned, gathered, quant, mult, done = [at(s - d) for d in (0, 1, 3, 4, 5, 7, 8)]
-            if s == 1:
-                nc.scalar.copy(out=gam_rows[:], in_=gam_ps[:])
+        for s in range(len(units) + 7):
+            new, norm, turned, gathered, quant, mult, done = [at(s - d) for d in (0, 1, 2, 3, 4, 6, 7)]
+            if gathered and gathered["r"] == 0:
+                gathered["chunk"]["grouped"] = work.tile(
+                    [P, 4 * DIN], BF16, name="grouped", tag="grouped", align_bytes=64
+                )
             if norm:
+                norm["xn"] = npool.tile([P, UNIT, DIN], BF16, name="xn", tag="xn")
                 times_rstd(norm)
+                times_rstd_only(norm)
             if new:
                 times_gamma(new)
                 square(new, 0)
-            if gathered and not on_vector(gathered, 0):
-                gather(gathered, 0)
             if new:
                 square(new, 1)
+            gather(gathered, 0, False)
+            gather(gathered, 1, False)
+            if new:
                 root(new)
-            if s in (4, 5):
-                gather_weights(s - 4, 0)
-                gather_weights(s - 4, 1)
             if norm:
                 normalise(norm, 0)
             if s == 1:
+                trace()
+            if s == 2:
+                threshold()
+                nc.vector.tensor_copy(out=gam_rows[:], in_=gam_ps[:])
                 ternary_masks()
-            if quant:
-                quantise(quant)
-            if s == 6:
+            if s in (3, 4):
+                gather_weights(s - 3)
+            if s == 5:
                 quantise_weights()
             if norm:
                 normalise(norm, 1)
-            if s == 5:
+            if s == 3:
+                nc.vector.tensor_copy(out=gam_k[:].rearrange("p g t -> p (g t)"), in_=gam_turned[0][:, :, 0])
+            if s == 4:
                 for i in range(UNIT):
                     nc.vector.tensor_copy(out=bias2[:, i * DOUT : (i + 1) * DOUT], in_=bias_ps[:])
-            if gathered and on_vector(gathered, 0):
-                gather(gathered, 0)
-            if gathered:
-                gather(gathered, 1)
+            gather(gathered, 0, True)
+            gather(gathered, 1, True)
             if done:
                 add_bias(done)
+            if quant:
+                quantise(quant)
             if turned:
                 turn(turned)
-            if s in (3, 4):
-                turn_weights(s - 3, 0)
-                turn_weights(s - 3, 1)
+            if s == 2:
+                turn_gamma()
+            if s in (2, 3):
+                turn_weights(s - 2)
             if mult:
                 multiply(mult)
             if done:

@@ -37,7 +37,7 @@ def tile_bitlinear_t_kernel(tc, x, weight, bias, gamma, out):
         npool = ctx.enter_context(tc.tile_pool(name="npool", bufs=4))
         work = ctx.enter_context(tc.tile_pool(name="work", bufs=3))
         small = ctx.enter_context(tc.tile_pool(name="small", bufs=4))
-        ps_t = ctx.enter_context(tc.psum_pool(name="ps_t", bufs=4))
+        ps_t = ctx.enter_context(tc.psum_pool(name="ps_t", bufs=5))
         ps_g = ctx.enter_context(tc.psum_pool(name="ps_g", bufs=1))
         ps_o = ctx.enter_context(tc.psum_pool(name="ps_o", bufs=2))
 
@@ -97,10 +97,10 @@ def tile_bitlinear_t_kernel(tc, x, weight, bias, gamma, out):
             return range(u["size"])
 
         def on_gpsimd(u, i):
-            return u["n"] == 4 and u["r"] + i == 0
+            return u["n"] > 1 and u["base"] > 2 and u["r"] + i == 0
 
         def on_vector(u, i):
-            return late_gamma(u, i) or u["base"] < 32 and u["base"] % 8 == 4 and u["r"] + i == 1
+            return late_gamma(u, i) or u["r"] + i == 3 and u["base"] < 24
 
         def late_gamma(u, i):
             return u["n"] == 4 and u["r"] + i == 2
@@ -221,27 +221,23 @@ def tile_bitlinear_t_kernel(tc, x, weight, bias, gamma, out):
 
         load(units[0])
         nc.sync.dma_start(out=vec_rows[0:8, :], in_=gamma.rearrange("(a k) -> a k", k=P))
-        nc.sync.dma_start(out=vec_rows[8:10, :], in_=bias.rearrange("(a k) -> a k", k=P))
         for u in units[1:3]:
             load(u)
         nc.sync.dma_start(out=w_sb[:], in_=weight.rearrange("(h p) k -> p h k", p=P))
         load(units[3])
+        gam_rows = const.tile([P, DIN], BF16)
+        nc.sync.dma_start(out=gam_rows[:], in_=gamma.partition_broadcast(P))
+        bias_bf = const.tile([P, DOUT], BF16)
+        nc.sync.dma_start(out=bias_bf[:], in_=bias.partition_broadcast(P))
 
         vec_ps = ps_t.tile([P, P], BF16, name="vec_ps", tag="pt")
         nc.tensor.transpose(out=vec_ps[:], in_=vec_rows[:], identity=ident[:])
-        vec_cols = const.tile([P, 10], BF16)
-        nc.vector.tensor_copy(out=vec_cols[:], in_=vec_ps[:, 0:10])
+        vec_cols = const.tile([P, 8], BF16)
+        nc.vector.tensor_copy(out=vec_cols[:], in_=vec_ps[:, 0:8])
         gam_ps = ps_g.tile([P, DIN], BF16)
         for a in range(8):
             nc.tensor.transpose(
                 out=gam_ps[:, a * P : (a + 1) * P], in_=vec_cols[:, a : a + 1].to_broadcast([P, P]), identity=ident[:]
-            )
-        gam_rows = const.tile([P, DIN], BF16)
-        bias_ps = ps_g.tile([P, DOUT], BF16, name="bias_ps", tag="bias_ps")
-        for h in range(2):
-            nc.tensor.transpose(
-                out=bias_ps[:, h * P : (h + 1) * P], in_=vec_cols[:, 8 + h : 9 + h].to_broadcast([P, P]),
-                identity=ident[:],
             )
         gam_k = const.tile([P, PASSES, PACK], F32)
         bias2 = const.tile([P, UNIT * DOUT], F32)
@@ -350,7 +346,6 @@ def tile_bitlinear_t_kernel(tc, x, weight, bias, gamma, out):
                 trace()
             if s == 2:
                 threshold()
-                nc.vector.tensor_copy(out=gam_rows[:], in_=gam_ps[:])
                 ternary_masks()
             if s in (3, 4):
                 gather_weights(s - 3)
@@ -362,7 +357,7 @@ def tile_bitlinear_t_kernel(tc, x, weight, bias, gamma, out):
                 nc.vector.tensor_copy(out=gam_k[:].rearrange("p g t -> p (g t)"), in_=gam_turned[0][:, :, 0])
             if s == 4:
                 for i in range(UNIT):
-                    nc.vector.tensor_copy(out=bias2[:, i * DOUT : (i + 1) * DOUT], in_=bias_ps[:])
+                    nc.vector.tensor_copy(out=bias2[:, i * DOUT : (i + 1) * DOUT], in_=bias_bf[:])
             gather(gathered, 0, True)
             gather(gathered, 1, True)
             if done:

@@ -22,6 +22,7 @@ EPS = 2.0 ** -23
 PASSES = 2
 PACK = 4
 CHUNKS = [1, 1, 2] + [4] * 14 + [2, 1, 1]
+VECTOR_COLS = 128
 UNIT = 2
 
 
@@ -100,7 +101,7 @@ def tile_bitlinear_t_kernel(tc, x, weight, bias, gamma, out):
             return u["n"] > 1 and u["base"] > 2 and u["r"] + i == 0
 
         def on_vector(u, i):
-            return late_gamma(u, i) or u["r"] + i == 3 and u["base"] < 24
+            return late_gamma(u, i) or u["r"] + i == 3 and u["base"] < 16
 
         def late_gamma(u, i):
             return u["n"] == 4 and u["r"] + i == 2
@@ -120,22 +121,24 @@ def tile_bitlinear_t_kernel(tc, x, weight, bias, gamma, out):
                 if on_gpsimd(u, i):
                     u["xg"] = work.tile([P, DIN], F32, name="xg", tag="xg")
                     nc.gpsimd.tensor_tensor(
-                        out=u["xg"][:], in0=chunk_of[u["base"]][:, u["r"] + i, :], in1=gam_rows[:], op=ALU.mult
+                        out=u["xg"][:, VECTOR_COLS:], in0=chunk_of[u["base"]][:, u["r"] + i, VECTOR_COLS:],
+                        in1=gam_rows[:, VECTOR_COLS:], op=ALU.mult,
                     )
 
         def times_rstd(u):
             for i in tiles(u):
                 if on_gpsimd(u, i):
                     nc.gpsimd.tensor_scalar(
-                        out=u["xn"][:, i, :], in0=u["xg"][:], scalar1=u["rstd"][:, i : i + 1], scalar2=1.0,
-                        op0=ALU.mult, op1=ALU.mult,
+                        out=u["xn"][:, i, VECTOR_COLS:], in0=u["xg"][:, VECTOR_COLS:],
+                        scalar1=u["rstd"][:, i : i + 1], scalar2=1.0, op0=ALU.mult, op1=ALU.mult,
                     )
 
         def normalise(u, i):
-            if i < u["size"] and not on_gpsimd(u, i) and not late_gamma(u, i):
+            if i < u["size"] and not late_gamma(u, i):
+                cols = slice(0, VECTOR_COLS if on_gpsimd(u, i) else DIN)
                 nc.vector.scalar_tensor_tensor(
-                    out=u["xn"][:, i, :], in0=chunk_of[u["base"]][:, u["r"] + i, :],
-                    scalar=u["rstd"][:, i : i + 1], in1=gam_ps[:], op0=ALU.mult, op1=ALU.mult,
+                    out=u["xn"][:, i, cols], in0=chunk_of[u["base"]][:, u["r"] + i, cols],
+                    scalar=u["rstd"][:, i : i + 1], in1=gam_ps[:, cols], op0=ALU.mult, op1=ALU.mult,
                 )
 
         def turn(u):

from contextlib import ExitStack

import concourse.mybir as mybir
from concourse.masks import make_identity

FLOPS = 2 * 8192 * 1024 * 256

BF16 = mybir.dt.bfloat16
F32 = mybir.dt.float32
U8 = mybir.dt.uint8
U32 = mybir.dt.uint32
FP8X4 = mybir.dt.float8_e4m3fn_x4
ALU = mybir.AluOpType
ACT = mybir.ActivationFunctionType
AX = mybir.AxisListType

P = 128
DIN = 1024
DOUT = 256
ROWS = 8192
EPS = 2.0 ** -23
PASSES = 2
PACK = 4
CHUNKS = [1, 1, 2] + [4] * 14 + [2, 1, 1]
VECTOR_COLS = 128
UNIT = 2


def tile_bitlinear_t_kernel(tc, x, weight, bias, gamma, out):
    nc = tc.nc
    assert sum(CHUNKS) * P == ROWS
    x_rows = x.flatten_outer_dims()
    out_rows = out.flatten_outer_dims()

    with ExitStack() as ctx:
        const = ctx.enter_context(tc.tile_pool(name="const", bufs=1))
        xpool = ctx.enter_context(tc.tile_pool(name="xpool", bufs=4))
        npool = ctx.enter_context(tc.tile_pool(name="npool", bufs=4))
        work = ctx.enter_context(tc.tile_pool(name="work", bufs=3))
        small = ctx.enter_context(tc.tile_pool(name="small", bufs=4))
        ps_t = ctx.enter_context(tc.psum_pool(name="ps_t", bufs=5))
        ps_g = ctx.enter_context(tc.psum_pool(name="ps_g", bufs=1))
        ps_o = ctx.enter_context(tc.psum_pool(name="ps_o", bufs=2))

        ctx.enter_context(tc.manual_schedule())

        warm = const.tile([P, 1], F32)
        nc.vector.memset(warm[:], 1.0)
        nc.scalar.activation(out=warm[:], in_=warm[:], func=ACT.Abs_reciprocal_sqrt)
        vec_rows = const.tile([P, P], BF16)
        nc.vector.memset(vec_rows[:], 0.0)
        w_sb = const.tile([P, 2, DIN], BF16)
        ident = const.tile([P, P], BF16)
        make_identity(nc, ident[:])
        neg_ident = const.tile([P, P], BF16)
        nc.vector.tensor_scalar(out=neg_ident[:], in0=ident[:], scalar1=-1.0, scalar2=None, op0=ALU.mult)
        ident_f32 = const.tile([P, P], F32)
        nc.vector.tensor_copy(out=ident_f32[:], in_=ident[:])
        ones = const.tile([P, P], F32)
        nc.vector.memset(ones[:], 1.0)

        units = []
        row_tile = 0
        for n in CHUNKS:
            chunk = {}
            for r in range(0, n, UNIT):
                units.append({"base": row_tile, "n": n, "r": r, "size": min(UNIT, n - r), "chunk": chunk})
            row_tile += n
        chunk_of = {}

        def load(u):
            if u["r"] > 0:
                return
            xs = xpool.tile([P, 4, DIN], BF16, name="xs", tag="xs")
            n = u["n"]
            rows = x_rows[u["base"] * P : (u["base"] + n) * P].rearrange("(p r) k -> p r k", r=n)
            nc.sync.dma_start(out=xs[:, 0:n, :], in_=rows)
            chunk_of[u["base"]] = xs

        def square(u, i):
            if i == 0:
                u["ssq"] = small.tile([P, UNIT], F32, name="ssq", tag="ssq")
            if i < u["size"]:
                sq = small.tile([P, DIN], BF16, name="sq", tag="sq")
                nc.scalar.activation(
                    out=sq[:], in_=chunk_of[u["base"]][:, u["r"] + i, :], func=ACT.Square,
                    accum_out=u["ssq"][:, i : i + 1],
                )

        def root(u):
            u["rstd"] = small.tile([P, UNIT], F32, name="rstd", tag="rstd")
            nc.scalar.activation(
                out=u["rstd"][:, 0 : u["size"]], in_=u["ssq"][:, 0 : u["size"]], func=ACT.Abs_reciprocal_sqrt,
                scale=1.0 / DIN, bias=EPS,
            )

        def tiles(u):
            return range(u["size"])

        def on_gpsimd(u, i):
            return u["n"] > 1 and u["base"] > 2 and u["r"] + i == 0

        def on_vector(u, i):
            return late_gamma(u, i) or u["r"] + i == 3 and u["base"] < 16

        def late_gamma(u, i):
            return u["n"] == 4 and u["r"] + i == 2

        def times_rstd_only(u):
            for i in tiles(u):
                if late_gamma(u, i):
                    u["xr"] = work.tile([P, DIN], F32, name="xr", tag="grouped", align_bytes=64)
                    nc.gpsimd.tensor_scalar(
                        out=u["xr"][:].rearrange("p (a e q) -> p a e q", a=4, e=2),
                        in0=chunk_of[u["base"]][:, u["r"] + i, :].rearrange("p (a q e) -> p a e q", a=4, e=2),
                        scalar1=u["rstd"][:, i : i + 1], scalar2=1.0, op0=ALU.mult, op1=ALU.mult,
                    )

        def times_gamma(u):
            for i in tiles(u):
                if on_gpsimd(u, i):
                    u["xg"] = work.tile([P, DIN], F32, name="xg", tag="xg")
                    nc.gpsimd.tensor_tensor(
                        out=u["xg"][:, VECTOR_COLS:], in0=chunk_of[u["base"]][:, u["r"] + i, VECTOR_COLS:],
                        in1=gam_rows[:, VECTOR_COLS:], op=ALU.mult,
                    )

        def times_rstd(u):
            for i in tiles(u):
                if on_gpsimd(u, i):
                    nc.gpsimd.tensor_scalar(
                        out=u["xn"][:, i, VECTOR_COLS:], in0=u["xg"][:, VECTOR_COLS:],
                        scalar1=u["rstd"][:, i : i + 1], scalar2=1.0, op0=ALU.mult, op1=ALU.mult,
                    )

        def normalise(u, i):
            if i < u["size"] and not late_gamma(u, i):
                cols = slice(0, VECTOR_COLS if on_gpsimd(u, i) else DIN)
                nc.vector.scalar_tensor_tensor(
                    out=u["xn"][:, i, cols], in0=chunk_of[u["base"]][:, u["r"] + i, cols],
                    scalar=u["rstd"][:, i : i + 1], in1=gam_ps[:, cols], op0=ALU.mult, op1=ALU.mult,
                )

        def turn(u):
            u["pt"] = []
            for i in tiles(u):
                if late_gamma(u, i):
                    pair = []
                    for g in range(PASSES):
                        pt = ps_t.tile([P, PACK, P], F32, name="pt", tag="pt")
                        for t in range(PACK):
                            c0 = (PACK * g + t) * P
                            nc.tensor.transpose(out=pt[:, t, :], in_=u["xr"][:, c0 : c0 + P], identity=ident_f32[:])
                        pair.append(pt)
                    u["pt"].append(pair)
                    continue
                words = u["xn"][:, i, :].bitcast(F32)
                pt = ps_t.tile([P, PASSES, 2, P], F32, name="pt", tag="pt")
                for g in range(PASSES):
                    for h in range(2):
                        w0 = (2 * g + h) * P
                        nc.tensor.transpose(out=pt[:, g, h, :], in_=words[:, w0 : w0 + P], identity=ident_f32[:])
                u["pt"].append(pt)

        def gather(u, i, vector):
            if u and i < u["size"] and on_vector(u, i) == vector:
                r = u["r"] + i
                if late_gamma(u, i):
                    for g in range(PASSES):
                        c0 = r * DIN + g * P * PACK
                        nc.vector.tensor_tensor(
                            out=u["chunk"]["grouped"][:, c0 : c0 + P * PACK].rearrange("p (m t) -> p m t", t=PACK),
                            in0=u["pt"][i][g][:].rearrange("p t m -> p m t"),
                            in1=gam_k[:, g, :].unsqueeze(1).to_broadcast([P, P, PACK]), op=ALU.mult,
                        )
                    return
                copy = nc.vector.tensor_copy if vector else nc.scalar.copy
                copy(
                    out=u["chunk"]["grouped"][:, r * DIN : (r + 1) * DIN].bitcast(F32).rearrange(
                        "p (g m h) -> p g m h", g=PASSES, h=2
                    ),
                    in_=u["pt"][i][:].rearrange("p g h m -> p g m h"),
                )

        def quantise(u):
            if u["r"] + u["size"] < u["n"]:
                return
            codes = work.tile([P, 4 * PASSES * P], U32, name="codes", tag="codes", align_bytes=64)
            scales = work.tile([P, 4 * PASSES * P], U8, name="scales", tag="scales", align_bytes=64)
            width = u["n"] * PASSES * P
            nc.vector.quantize_mx(
                out=codes[:, 0:width].bitcast(FP8X4), scales=scales[:, 0:width],
                in_=u["chunk"]["grouped"][:, 0 : width * PACK],
            )
            u["chunk"]["codes"], u["chunk"]["scales"] = codes, scales

        def multiply(u):
            u["po"] = ps_o.tile([P, UNIT * DOUT], F32, name="po", tag="po")
            for i in tiles(u):
                for g in range(PASSES):
                    word0 = (PASSES * (u["r"] + i) + g) * P
                    rows = slice(word0, word0 + P)
                    ch = slice(g * DOUT, (g + 1) * DOUT)
                    nc.tensor.matmul_mx(
                        out=u["po"][:, i * DOUT : (i + 1) * DOUT],
                        lhsT=u["chunk"]["codes"][:, rows].bitcast(FP8X4), lhsT_scale=u["chunk"]["scales"][:, rows],
                        rhs=w_codes[:, ch].bitcast(FP8X4), rhs_scale=w_scales[:, ch],
                        start=(g == 0), stop=(g == PASSES - 1),
                    )

        def add_bias(u):
            u["o_sb"] = npool.tile([P, UNIT * DOUT], F32, name="o_sb", tag="o_sb")
            cols = slice(0, u["size"] * DOUT)
            nc.vector.tensor_tensor(out=u["o_sb"][:, cols], in0=u["po"][:, cols], in1=bias2[:, cols], op=ALU.add)

        def store(u):
            size = u["size"]
            n = u["n"]
            rows = out_rows[u["base"] * P : (u["base"] + n) * P].rearrange("(p r) c -> p r c", r=n)
            nc.sync.dma_start(
                out=rows[:, u["r"] : u["r"] + size, :],
                in_=u["o_sb"][:, 0 : size * DOUT].rearrange("p (i c) -> p i c", i=size),
            )

        load(units[0])
        nc.sync.dma_start(out=vec_rows[0:8, :], in_=gamma.rearrange("(a k) -> a k", k=P))
        for u in units[1:3]:
            load(u)
        nc.sync.dma_start(out=w_sb[:], in_=weight.rearrange("(h p) k -> p h k", p=P))
        load(units[3])
        gam_rows = const.tile([P, DIN], BF16)
        nc.sync.dma_start(out=gam_rows[:], in_=gamma.partition_broadcast(P))
        bias_bf = const.tile([P, DOUT], BF16)
        nc.sync.dma_start(out=bias_bf[:], in_=bias.partition_broadcast(P))

        vec_ps = ps_t.tile([P, P], BF16, name="vec_ps", tag="pt")
        nc.tensor.transpose(out=vec_ps[:], in_=vec_rows[:], identity=ident[:])
        vec_cols = const.tile([P, 8], BF16)
        nc.vector.tensor_copy(out=vec_cols[:], in_=vec_ps[:, 0:8])
        gam_ps = ps_g.tile([P, DIN], BF16)
        for a in range(8):
            nc.tensor.transpose(
                out=gam_ps[:, a * P : (a + 1) * P], in_=vec_cols[:, a : a + 1].to_broadcast([P, P]), identity=ident[:]
            )
        gam_k = const.tile([P, PASSES, PACK], F32)
        bias2 = const.tile([P, UNIT * DOUT], F32)

        half_sign = const.tile([P, 2 * DIN], BF16)
        gram = ps_o.tile([P, P], F32, name="gram", tag="po")

        def trace():
            nc.vector.tensor_scalar(
                out=half_sign[:], in0=w_sb[:].rearrange("p h k -> p (h k)"), scalar1=0.0, scalar2=0.5,
                op0=ALU.is_ge, op1=ALU.subtract,
            )
            for b in range(2 * DIN // P):
                nc.tensor.matmul(
                    gram[:], lhsT=w_sb[:].rearrange("p h k -> p (h k)")[:, b * P : (b + 1) * P],
                    rhs=half_sign[:, b * P : (b + 1) * P], start=(b == 0), stop=(b == 2 * DIN // P - 1),
                )

        thr = const.tile([P, 1], F32)
        nthr = const.tile([P, 1], F32)

        def threshold():
            diag = const.tile([P, P], F32)
            diag_sum = const.tile([P, 1], F32)
            nc.vector.scalar_tensor_tensor(
                out=diag[:], in0=gram[:], scalar=1.0, in1=ident_f32[:], op0=ALU.mult, op1=ALU.mult,
                accum_out=diag_sum[:],
            )
            tot = ps_o.tile([P, 1], F32, name="tot", tag="po")
            nc.tensor.matmul(tot[:], lhsT=ones[:], rhs=diag_sum[:], start=True, stop=True)
            mean = 2.0 / (DOUT * DIN)
            nc.vector.tensor_scalar(out=thr[:], in0=tot[:], scalar1=mean, scalar2=None, op0=ALU.mult)
            nc.vector.tensor_scalar(out=nthr[:], in0=tot[:], scalar1=-mean, scalar2=None, op0=ALU.mult)

        w_flat = w_sb[:].rearrange("p h k -> p (h k)")
        w_pos = const.tile([P, 2, DIN], BF16)
        w_neg = const.tile([P, 2, DIN], BF16)

        def ternary_masks():
            for mask, limit, op in ((w_pos, thr, ALU.is_gt), (w_neg, nthr, ALU.is_lt)):
                nc.vector.tensor_scalar(
                    out=mask[:].rearrange("p h k -> p (h k)"), in0=w_flat, scalar1=limit[:, 0:1], scalar2=None, op0=op
                )

        w_grouped = const.tile([P, PASSES, DOUT, PACK], BF16, align_bytes=64)
        w_codes = const.tile([P, PASSES * DOUT], U32, align_bytes=64)
        w_scales = const.tile([P, PASSES * DOUT], U8, align_bytes=64)

        gam_turned = []
        w_turned = {}

        def turn_gamma():
            gt = ps_o.tile([P, 2 * PACK, P], BF16, name="gt", tag="po")
            for j in range(2 * PACK):
                k0 = j // 2 * 2 * P + j % 2
                nc.tensor.transpose(out=gt[:, j, :], in_=gam_rows[:, k0 : k0 + 2 * P - 1 : 2], identity=ident[:])
            gam_turned.append(gt)

        def turn_weights(g):
            for h in range(2):
                w_ps = ps_t.tile([P, PACK, P], F32, name="w_ps", tag="pt")
                for t in range(PACK):
                    k0 = g * P * PACK + (t // 2) * 2 * P + t % 2
                    k_cols = slice(k0, k0 + 2 * P - 1, 2)
                    nc.tensor.matmul(w_ps[:, t, :], lhsT=w_pos[:, h, k_cols], rhs=ident[:], start=True, stop=False)
                    nc.tensor.matmul(w_ps[:, t, :], lhsT=w_neg[:, h, k_cols], rhs=neg_ident[:], start=False, stop=True)
                w_turned[g, h] = w_ps

        def gather_weights(g):
            for h in range(2):
                nc.vector.tensor_copy(
                    out=w_grouped[:, g, h * P : (h + 1) * P, :], in_=w_turned[g, h][:].rearrange("p t n -> p n t")
                )

        def quantise_weights():
            nc.vector.quantize_mx(
                out=w_codes[:].bitcast(FP8X4), scales=w_scales[:],
                in_=w_grouped[:].rearrange("p g n t -> p (g n t)"),
            )

        def at(i):
            return units[i] if 0 <= i < len(units) else None

        for s in range(len(units) + 7):
            new, norm, turned, gathered, quant, mult, done = [at(s - d) for d in (0, 1, 2, 3, 4, 6, 7)]
            if gathered and gathered["r"] == 0:
                gathered["chunk"]["grouped"] = work.tile(
                    [P, 4 * DIN], BF16, name="grouped", tag="grouped", align_bytes=64
                )
            if norm:
                norm["xn"] = npool.tile([P, UNIT, DIN], BF16, name="xn", tag="xn")
                times_rstd(norm)
                times_rstd_only(norm)
            if new:
                times_gamma(new)
                square(new, 0)
            if new:
                square(new, 1)
            gather(gathered, 0, False)
            gather(gathered, 1, False)
            if new:
                root(new)
            if norm:
                normalise(norm, 0)
            if s == 1:
                trace()
            if s == 2:
                threshold()
                ternary_masks()
            if s in (3, 4):
                gather_weights(s - 3)
            if s == 5:
                quantise_weights()
            if norm:
                normalise(norm, 1)
            if s == 3:
                nc.vector.tensor_copy(out=gam_k[:].rearrange("p g t -> p (g t)"), in_=gam_turned[0][:, :, 0])
            if s == 4:
                for i in range(UNIT):
                    nc.vector.tensor_copy(out=bias2[:, i * DOUT : (i + 1) * DOUT], in_=bias_bf[:])
            gather(gathered, 0, True)
            gather(gathered, 1, True)
            if done:
                add_bias(done)
            if quant:
                quantise(quant)
            if turned:
                turn(turned)
            if s == 2:
                turn_gamma()
            if s in (2, 3):
                turn_weights(s - 2)
            if mult:
                multiply(mult)
            if done:
                store(done)
            if s >= 1 and at(s + 3):
                load(at(s + 3))
